import numpy as np
import ml_dtypes


def mxq(x, axis, fmt="e4m3"):
    dtype, down = {"e4m3": (ml_dtypes.float8_e4m3fn, 7), "e5m2": (ml_dtypes.float8_e5m2, 14)}[fmt]
    v = np.moveaxis(np.asarray(x, np.float32).astype(ml_dtypes.bfloat16).astype(np.float64), axis, -1)
    blocks = v.reshape(v.shape[:-1] + (-1, 32))
    amax = np.abs(blocks).max(-1, keepdims=True)
    byte = np.maximum(np.where(amax > 0, np.frexp(amax)[1] - 1 + 127, 0) - down, 1)
    scale = np.exp2(byte - 127.0)
    codes = (blocks / scale).astype(np.float32).astype(dtype).astype(np.float64)
    return np.moveaxis((codes * scale).reshape(v.shape), -1, axis)


WIDE = False


def mx_kscale(k):
    if not WIDE:
        return np.ones(k)
    levels = np.array([10, -10, 5, -5, 0])
    a = np.random.permutation(np.resize(levels, k // 512 * 4)).reshape(k // 512, 4)
    idx = np.arange(k)
    return np.exp2(a[idx // 512, idx % 128 // 32])


BF16 = ml_dtypes.bfloat16


def bf(x):
    return np.asarray(x, np.float32).astype(BF16)


def f64(x):
    return np.asarray(x).astype(np.float64)


B, I, H = 4096, 512, 512
SPARSITY = 0.5
TS = 1.0


def erf(v):
    a = np.minimum(np.abs(v), 6.0)
    q = 2.0 * a * a
    term, total, n = a, a, 0
    while np.any(term > 1e-18 * total):
        n += 1
        term = term * (q / (2 * n + 1))
        total = total + term
    return np.sign(v) * total * np.exp(-a * a) * 2.0 / np.sqrt(np.pi)


def gelu(v):
    return 0.5 * v * (1.0 + erf(v / np.sqrt(2.0)))


def sigmoid(v):
    return 1.0 / (1.0 + np.exp(-v))


def setup_inputs():
    s, u = mx_kscale(H), mx_kscale(I)
    rn = np.random.standard_normal
    keep = np.random.random((H, H)) > SPARSITY
    return {"ff1": bf(gelu(rn((B, H))) * s), "x": bf(rn((B, I)) * u), "hx": bf(rn((B, H))),
            "W_ff2": bf(rn((H, H)) * 1.5 / np.sqrt(H) / s), "b_ff2": bf(rn(H) * 0.3),
            "W_ta": bf(rn((H, H)) * 1.5 / np.sqrt(H)), "b_ta": bf(rn(H) * 0.3),
            "W_tb": bf(rn((H, H)) * 1.5 / np.sqrt(H)), "b_tb": bf(rn(H) * 0.3),
            "W_in": bf(rn((H, I)) / np.sqrt(I) / u), "b_in": bf(rn(H) * 0.3), "input_b": bf(rn(H) * 0.3),
            "W_r": bf(rn((H, H)) * keep / np.sqrt((1.0 - SPARSITY) * H)), "r_b": bf(rn(H) * 0.3)}


def reference(ff1, x, hx, W_ff2, b_ff2, W_ta, b_ta, W_tb, b_tb, W_in, b_in, input_b, W_r, r_b):
    h0 = f64(hx)
    ff2 = gelu((mxq(f64(ff1), 1, "e4m3") @ mxq(f64(W_ff2), 1, "e4m3").T) + f64(b_ff2))
    ff2q = mxq(ff2, 1, "e4m3")
    t_a = (ff2q @ mxq(f64(W_ta), 1, "e4m3").T) + f64(b_ta)
    t_b = (ff2q @ mxq(f64(W_tb), 1, "e4m3").T) + f64(b_tb)
    t_interp = sigmoid(t_a * TS + t_b)
    input_contrib = gelu((mxq(f64(x), 1, "e4m3") @ mxq(f64(W_in), 1, "e4m3").T) + f64(b_in) + f64(input_b))
    recurrent_contrib = gelu((mxq(h0, 1, "e4m3") @ mxq(f64(W_r), 1, "e4m3").T) + f64(r_b))
    return h0 * (1.0 - t_interp) + t_interp * (input_contrib + recurrent_contrib)

@@ -1,0 +1,264 @@
+from contextlib import ExitStack
+
+import concourse.mybir as mybir
+from concourse.masks import make_identity
+
+F32 = mybir.dt.float32
+BF16 = mybir.dt.bfloat16
+U32 = mybir.dt.uint32
+U8 = mybir.dt.uint8
+FP8X4 = mybir.dt.float8_e4m3fn_x4
+ACT = mybir.ActivationFunctionType
+ALU = mybir.AluOpType
+
+P = 128
+PACK = 4
+B = 4096
+H = 512
+GROUP = 512
+BLOCKS = GROUP // P
+CHUNKS = H // P
+N_GROUPS = B // GROUP
+WORDS = H // 2
+
+FLOPS = 5 * 2 * B * H * H
+
+
+def transpose_and_quantise(nc, pools, rows, ident, copy, codes, scales, grouped_tag):
+    words = rows.bitcast(F32)
+    grouped = pools["grouped"].tile([P, GROUP * PACK], BF16, align_bytes=64, tag=grouped_tag, name=grouped_tag)
+    grouped_words = grouped[:].bitcast(F32).rearrange("p (c u) -> p c u", u=2)
+    half_cols = GROUP // 2
+    for half in range(2):
+        planes = pools["psum_t"].tile([P, 2, half_cols], F32, tag="transposed", name="planes")
+        for s in range(2):
+            slot = 2 * half + s
+            for u in range(2):
+                nc.tensor.transpose(
+                    planes[:, u, s * P : (s + 1) * P],
+                    words[:, slot * WORDS + u * P : slot * WORDS + (u + 1) * P],
+                    ident,
+                )
+        copy(
+            out=grouped_words[:, half * half_cols : (half + 1) * half_cols, :],
+            in_=planes[:].rearrange("p u c -> p c u"),
+        )
+    nc.vector.quantize_mx(out=codes.bitcast(FP8X4), scales=scales, in_=grouped[:])
+    return grouped
+
+
+def tile_cfccell_pa_t_kernel(
+    tc, ff1, x, hx, W_ff2, b_ff2, W_ta, b_ta, W_tb, b_tb, W_in, b_in, input_b, W_r, r_b, out
+):
+    nc = tc.nc
+    with ExitStack() as stack:
+        pools = {
+            "const": stack.enter_context(tc.tile_pool(name="const", bufs=1)),
+            "rows": stack.enter_context(tc.tile_pool(name="rows", bufs=3)),
+            "grouped": stack.enter_context(tc.tile_pool(name="grouped", bufs=2)),
+            "mx": stack.enter_context(tc.tile_pool(name="mx", bufs=2)),
+            "work": stack.enter_context(tc.tile_pool(name="work", bufs=2)),
+            "store": stack.enter_context(tc.tile_pool(name="store", bufs=6)),
+            "psum_t": stack.enter_context(tc.psum_pool(name="psum_t", bufs=4)),
+            "psum_mx": stack.enter_context(tc.psum_pool(name="psum_mx", bufs=4)),
+        }
+        const = pools["const"]
+        stack.enter_context(tc.manual_schedule())
+
+        warm_in = const.tile([P, 1], F32)
+        warm_out = const.tile([P, 1], F32)
+        nc.vector.memset(warm_in[:], 0.0)
+        nc.scalar.activation(out=warm_out[:], in_=warm_in[:], func=ACT.Gelu)
+
+        ident = const.tile([P, P], F32)
+        make_identity(nc, ident[:])
+
+        def load_group(g):
+            tiles = {}
+            for name, src, bufs in (("ff1", ff1, 3), ("x", x, 3), ("hx", hx, 3)):
+                tiles[name] = pools["rows"].tile([P, BLOCKS * H], BF16, tag=name, bufs=bufs, name=name)
+                nc.sync.dma_start(
+                    out=tiles[name][:],
+                    in_=src.rearrange("(g p s) k -> g p (s k)", p=P, s=BLOCKS)[g],
+                )
+            return tiles
+
+        def load_weight(name, w):
+            tile = const.tile([P, CHUNKS * H], BF16, name="rows_" + name)
+            nc.sync.dma_start(
+                out=tile[:].rearrange("r (u ek) -> r u ek", u=2),
+                in_=w.rearrange("(u r e) k -> r u (e k)", u=2, e=2),
+            )
+            return tile
+
+        weight_rows = {"ff2": load_weight("ff2", W_ff2)}
+        group_rows = load_group(0)
+        for name, w in (("in", W_in), ("ta", W_ta), ("tb", W_tb), ("r", W_r)):
+            weight_rows[name] = load_weight(name, w)
+
+        vectors = (b_ff2, b_ta, b_tb, b_in, input_b, r_b)
+        bias_rows = const.tile([P, H], BF16)
+        nc.vector.memset(bias_rows[:], 0.0)
+        for v, vec in enumerate(vectors):
+            nc.scalar.dma_start(out=bias_rows[v : v + 1, :], in_=vec.rearrange("(o h) -> o h", o=1))
+        bias_planes = pools["psum_t"].tile([P, 2, P], F32, tag="transposed", name="bias_planes")
+        for u in range(2):
+            nc.tensor.transpose(
+                bias_planes[:, u, :], bias_rows[:].bitcast(F32)[:, u * P : (u + 1) * P], ident[:]
+            )
+        bias = const.tile([P, len(vectors), CHUNKS], F32)
+        nc.vector.tensor_copy(
+            out=bias[:].rearrange("p v (u e) -> p v u e", e=2),
+            in_=bias_planes[:].bitcast(BF16)[:, :, 0 : 2 * len(vectors)].rearrange(
+                "p u (v e) -> p v u e", e=2
+            ),
+        )
+        bias_ff2 = bias[:, 0, :]
+        bias_rec = bias[:, 5, :]
+        bias_in = const.tile([P, CHUNKS], F32)
+        nc.vector.tensor_tensor(out=bias_in[:], in0=bias[:, 3, :], in1=bias[:, 4, :], op=ALU.add)
+        bias_gate_sum = const.tile([P, CHUNKS], F32)
+        bias_gate = const.tile([P, CHUNKS], F32)
+        nc.vector.tensor_tensor(out=bias_gate_sum[:], in0=bias[:, 1, :], in1=bias[:, 2, :], op=ALU.add)
+        nc.vector.tensor_scalar_mul(out=bias_gate[:], in0=bias_gate_sum[:], scalar1=0.5)
+
+        w_codes = {}
+        w_scales = {}
+
+        def prepare_weight(name):
+            w_codes[name] = const.tile([P, H], U32, align_bytes=64, name="codes_" + name)
+            w_scales[name] = const.tile([P, H], U8, align_bytes=64, name="scales_" + name)
+            transpose_and_quantise(
+                nc, pools, weight_rows[name][:], ident[:], nc.vector.tensor_copy,
+                w_codes[name][:], w_scales[name][:], "grouped",
+            )
+
+        def quantise_rows(name, rows, grouped_tag):
+            codes = pools["mx"].tile([P, GROUP], U32, align_bytes=64, tag="codes_" + name, name="codes_" + name)
+            scales = pools["mx"].tile([P, GROUP], U8, align_bytes=64, tag="scales_" + name, name="scales_" + name)
+            grouped = transpose_and_quantise(
+                nc, pools, rows[:], ident[:], nc.scalar.copy, codes[:], scales[:], grouped_tag
+            )
+            return codes, scales, grouped
+
+        def product(c, terms):
+            acc = pools["psum_mx"].tile([P, GROUP], F32, tag="acc", name="acc")
+            for i, (weight, codes, scales) in enumerate(terms):
+                nc.tensor.matmul_mx(
+                    out=acc[:],
+                    lhsT=w_codes[weight][:, c * P : (c + 1) * P].bitcast(FP8X4),
+                    lhsT_scale=w_scales[weight][:, c * P : (c + 1) * P],
+                    rhs=codes[:].bitcast(FP8X4),
+                    rhs_scale=scales[:],
+                    start=(i == 0),
+                    stop=(i == len(terms) - 1),
+                )
+            return acc
+
+        out_groups = out.rearrange("(g p s) f -> g p s f", p=P, s=BLOCKS)
+
+        live = {}
+
+        def prepare(name, g, grouped_tag):
+            live[g][name] = quantise_rows(name, live[g]["rows"][name], grouped_tag)
+
+        def hidden_layer(g):
+            codes, scales, grouped = live[g]["ff1"]
+            ff2 = pools["work"].tile([P, CHUNKS, GROUP], BF16, name="ff2")
+            for c in range(CHUNKS):
+                acc = product(c, [("ff2", codes, scales)])
+                nc.scalar.activation(out=ff2[:, c, :], in_=acc[:], func=ACT.Gelu, bias=bias_ff2[:, c : c + 1])
+            ff2_grouped = pools["grouped"].tile([P, GROUP * PACK], BF16, align_bytes=64, name="ff2_grouped")
+            nc.vector.tensor_copy(
+                out=ff2_grouped[:].rearrange("p (b i j) -> p b j i", i=4, j=PACK),
+                in_=ff2[:].rearrange("p j (b i) -> p b j i", i=4),
+            )
+            ff2_codes = pools["mx"].tile([P, GROUP], U32, align_bytes=64, name="ff2_codes")
+            ff2_scales = pools["mx"].tile([P, GROUP], U8, align_bytes=64, name="ff2_scales")
+            nc.vector.quantize_mx(out=ff2_codes[:].bitcast(FP8X4), scales=ff2_scales[:], in_=ff2_grouped[:])
+            live[g]["ff2"] = (ff2_codes, ff2_scales)
+
+        def input_part(g):
+            codes, scales, grouped = live[g]["x"]
+            delta = pools["work"].tile([P, CHUNKS, GROUP], F32, name="delta")
+            for c in range(CHUNKS):
+                acc = product(c, [("in", codes, scales)])
+                nc.scalar.activation(out=delta[:, c, :], in_=acc[:], func=ACT.Gelu, bias=bias_in[:, c : c + 1])
+            live[g]["delta"] = delta
+
+        def subtract_state(g):
+            delta = live[g]["delta"]
+            grouped = live[g]["hx"][2]
+            nc.vector.tensor_tensor(
+                out=delta[:], in0=delta[:], in1=grouped[:].rearrange("p (b j) -> p j b", j=PACK), op=ALU.subtract
+            )
+
+        def gate_part(g):
+            codes, scales = live[g]["ff2"]
+            gate = pools["work"].tile([P, CHUNKS, GROUP], F32, name="gate")
+            for c in range(CHUNKS):
+                acc = product(c, [("ta", codes, scales), ("tb", codes, scales)])
+                nc.scalar.activation(
+                    out=gate[:, c, :], in_=acc[:], func=ACT.Tanh, bias=bias_gate[:, c : c + 1], scale=0.5
+                )
+            live[g]["gate"] = gate
+
+        def recurrent_part(g):
+            codes, scales, grouped = live[g]["hx"]
+            delta = live[g]["delta"]
+            gate = live[g]["gate"]
+            rec = pools["work"].tile([P, CHUNKS, GROUP], F32, name="rec")
+            for c in range(CHUNKS):
+                acc = product(c, [("r", codes, scales)])
+                nc.scalar.activation(out=rec[:, c, :], in_=acc[:], func=ACT.Gelu, bias=bias_rec[:, c : c + 1])
+            for pair in range(2):
+                chunks = slice(2 * pair, 2 * pair + 2)
+                nc.vector.tensor_tensor(out=delta[:, chunks, :], in0=delta[:, chunks, :], in1=rec[:, chunks, :], op=ALU.add)
+            for pair in range(2):
+                cols = slice(2 * pair * P, (2 * pair + 2) * P)
+                nc.vector.scalar_tensor_tensor(
+                    out=delta[:, :, cols], in0=gate[:, :, cols], scalar=1.0, in1=delta[:, :, cols],
+                    op0=ALU.add, op1=ALU.mult,
+                )
+
+        def blend_and_store(g):
+            delta = live[g]["delta"]
+            hx_rows = live[g]["rows"]["hx"]
+            for s in range(BLOCKS):
+                back = pools["psum_t"].tile([P, H], F32, tag="transposed", name="back")
+                for c in range(CHUNKS):
+                    u, e = divmod(c, 2)
+                    nc.tensor.transpose(
+                        back[:, e * WORDS + u * P : e * WORDS + (u + 1) * P], delta[:, c, s * P : (s + 1) * P], ident[:]
+                    )
+                result = pools["store"].tile([P, H], F32, name="result")
+                nc.vector.scalar_tensor_tensor(
+                    out=result[:].rearrange("b (q e) -> b q e", e=2),
+                    in0=back[:].rearrange("b (e q) -> b q e", e=2),
+                    scalar=0.5,
+                    in1=hx_rows[:, s * H : (s + 1) * H].rearrange("b (q e) -> b q e", e=2),
+                    op0=ALU.mult,
+                    op1=ALU.add,
+                )
+                nc.sync.dma_start(out=out_groups[g][:, s, :], in_=result[:])
+
+        live[0] = {"rows": group_rows}
+        prepare_weight("ff2")
+        prepare("ff1", 0, "grouped")
+        for name in ("in", "ta", "tb", "r"):
+            prepare_weight(name)
+        for g in range(N_GROUPS):
+            if g + 1 < N_GROUPS:
+                live[g + 1] = {"rows": load_group(g + 1)}
+            prepare("x", g, "grouped")
+            hidden_layer(g)
+            prepare("hx", g, "hx_grouped")
+            input_part(g)
+            if g > 0:
+                blend_and_store(g - 1)
+            subtract_state(g)
+            gate_part(g)
+            if g + 1 < N_GROUPS:
+                prepare("ff1", g + 1, "grouped")
+            recurrent_part(g)
+        blend_and_store(N_GROUPS - 1)

@@ -54,7 +54,7 @@ def tile_cfccell_pa_t_kernel(
     with ExitStack() as stack:
         pools = {
             "const": stack.enter_context(tc.tile_pool(name="const", bufs=1)),
-            "rows": stack.enter_context(tc.tile_pool(name="rows", bufs=3)),
+            "rows": stack.enter_context(tc.tile_pool(name="rows", bufs=4)),
             "grouped": stack.enter_context(tc.tile_pool(name="grouped", bufs=2)),
             "mx": stack.enter_context(tc.tile_pool(name="mx", bufs=2)),
             "work": stack.enter_context(tc.tile_pool(name="work", bufs=2)),
@@ -73,10 +73,16 @@ def tile_cfccell_pa_t_kernel(
         ident = const.tile([P, P], F32)
         make_identity(nc, ident[:])
 
+        vectors = (b_ff2, b_ta, b_tb, b_in, input_b, r_b)
+        bias_rows = const.tile([P, H], BF16)
+        nc.vector.memset(bias_rows[:], 0.0)
+        for v, vec in enumerate(vectors):
+            nc.scalar.dma_start(out=bias_rows[v : v + 1, :], in_=vec.rearrange("(o h) -> o h", o=1))
+
         def load_group(g):
             tiles = {}
-            for name, src, bufs in (("ff1", ff1, 3), ("x", x, 3), ("hx", hx, 3)):
-                tiles[name] = pools["rows"].tile([P, BLOCKS * H], BF16, tag=name, bufs=bufs, name=name)
+            for name, src in (("ff1", ff1), ("x", x), ("hx", hx)):
+                tiles[name] = pools["rows"].tile([P, BLOCKS * H], BF16, tag=name, name=name)
                 nc.sync.dma_start(
                     out=tiles[name][:],
                     in_=src.rearrange("(g p s) k -> g p (s k)", p=P, s=BLOCKS)[g],
@@ -91,16 +97,13 @@ def tile_cfccell_pa_t_kernel(
             )
             return tile
 
+        live = {}
         weight_rows = {"ff2": load_weight("ff2", W_ff2)}
-        group_rows = load_group(0)
-        for name, w in (("in", W_in), ("ta", W_ta), ("tb", W_tb), ("r", W_r)):
+        live[0] = {"rows": load_group(0)}
+        for name, w in (("in", W_in), ("r", W_r), ("ta", W_ta), ("tb", W_tb)):
             weight_rows[name] = load_weight(name, w)
+        live[1] = {"rows": load_group(1)}
 
-        vectors = (b_ff2, b_ta, b_tb, b_in, input_b, r_b)
-        bias_rows = const.tile([P, H], BF16)
-        nc.vector.memset(bias_rows[:], 0.0)
-        for v, vec in enumerate(vectors):
-            nc.scalar.dma_start(out=bias_rows[v : v + 1, :], in_=vec.rearrange("(o h) -> o h", o=1))
         bias_planes = pools["psum_t"].tile([P, 2, P], F32, tag="transposed", name="bias_planes")
         for u in range(2):
             nc.tensor.transpose(
@@ -157,7 +160,6 @@ def tile_cfccell_pa_t_kernel(
 
         out_groups = out.rearrange("(g p s) f -> g p s f", p=P, s=BLOCKS)
 
-        live = {}
 
         def prepare(name, g, grouped_tag):
             live[g][name] = quantise_rows(name, live[g]["rows"][name], grouped_tag)
@@ -193,31 +195,28 @@ def tile_cfccell_pa_t_kernel(
                 out=delta[:], in0=delta[:], in1=grouped[:].rearrange("p (b j) -> p j b", j=PACK), op=ALU.subtract
             )
 
+        def recurrent_part(g):
+            codes, scales, grouped = live[g]["hx"]
+            delta = live[g]["delta"]
+            rec = pools["work"].tile([P, CHUNKS, GROUP], F32, name="rec")
+            for c in range(CHUNKS):
+                acc = product(c, [("r", codes, scales)])
+                nc.scalar.activation(out=rec[:, c, :], in_=acc[:], func=ACT.Gelu, bias=bias_rec[:, c : c + 1])
+            for pair in (slice(0, 2), slice(2, 4)):
+                nc.vector.tensor_tensor(out=delta[:, pair, :], in0=delta[:, pair, :], in1=rec[:, pair, :], op=ALU.add)
+
         def gate_part(g):
             codes, scales = live[g]["ff2"]
+            delta = live[g]["delta"]
             gate = pools["work"].tile([P, CHUNKS, GROUP], F32, name="gate")
             for c in range(CHUNKS):
                 acc = product(c, [("ta", codes, scales), ("tb", codes, scales)])
                 nc.scalar.activation(
                     out=gate[:, c, :], in_=acc[:], func=ACT.Tanh, bias=bias_gate[:, c : c + 1], scale=0.5
                 )
-            live[g]["gate"] = gate
-
-        def recurrent_part(g):
-            codes, scales, grouped = live[g]["hx"]
-            delta = live[g]["delta"]
-            gate = live[g]["gate"]
-            rec = pools["work"].tile([P, CHUNKS, GROUP], F32, name="rec")
-            for c in range(CHUNKS):
-                acc = product(c, [("r", codes, scales)])
-                nc.scalar.activation(out=rec[:, c, :], in_=acc[:], func=ACT.Gelu, bias=bias_rec[:, c : c + 1])
-            for pair in range(2):
-                chunks = slice(2 * pair, 2 * pair + 2)
-                nc.vector.tensor_tensor(out=delta[:, chunks, :], in0=delta[:, chunks, :], in1=rec[:, chunks, :], op=ALU.add)
-            for pair in range(2):
-                cols = slice(2 * pair * P, (2 * pair + 2) * P)
+            for pair in (slice(0, 2), slice(2, 4)):
                 nc.vector.scalar_tensor_tensor(
-                    out=delta[:, :, cols], in0=gate[:, :, cols], scalar=1.0, in1=delta[:, :, cols],
+                    out=delta[:, pair, :], in0=gate[:, pair, :], scalar=1.0, in1=delta[:, pair, :],
                     op0=ALU.add, op1=ALU.mult,
                 )
 
@@ -242,23 +241,24 @@ def tile_cfccell_pa_t_kernel(
                 )
                 nc.sync.dma_start(out=out_groups[g][:, s, :], in_=result[:])
 
-        live[0] = {"rows": group_rows}
         prepare_weight("ff2")
         prepare("ff1", 0, "grouped")
-        for name in ("in", "ta", "tb", "r"):
+        prepare_weight("in")
+        prepare("x", 0, "grouped")
+        for name in ("r", "ta", "tb"):
             prepare_weight(name)
         for g in range(N_GROUPS):
-            if g + 1 < N_GROUPS:
-                live[g + 1] = {"rows": load_group(g + 1)}
-            prepare("x", g, "grouped")
+            if g + 2 < N_GROUPS:
+                live[g + 2] = {"rows": load_group(g + 2)}
             hidden_layer(g)
             prepare("hx", g, "hx_grouped")
             input_part(g)
-            if g > 0:
-                blend_and_store(g - 1)
             subtract_state(g)
-            gate_part(g)
             if g + 1 < N_GROUPS:
                 prepare("ff1", g + 1, "grouped")
+                prepare("x", g + 1, "grouped")
             recurrent_part(g)
+            if g > 0:
+                blend_and_store(g - 1)
+            gate_part(g)
         blend_and_store(N_GROUPS - 1)

@@ -20,6 +20,7 @@ BLOCKS = GROUP // P
 CHUNKS = H // P
 N_GROUPS = B // GROUP
 WORDS = H // 2
+CHUNK_PAIRS = (slice(0, 2), slice(2, 4))
 
 FLOPS = 5 * 2 * B * H * H
 
@@ -65,11 +66,6 @@ def tile_cfccell_pa_t_kernel(
         const = pools["const"]
         stack.enter_context(tc.manual_schedule())
 
-        warm_in = const.tile([P, 1], F32)
-        warm_out = const.tile([P, 1], F32)
-        nc.vector.memset(warm_in[:], 0.0)
-        nc.scalar.activation(out=warm_out[:], in_=warm_in[:], func=ACT.Gelu)
-
         ident = const.tile([P, P], F32)
         make_identity(nc, ident[:])
 
@@ -78,6 +74,11 @@ def tile_cfccell_pa_t_kernel(
         nc.vector.memset(bias_rows[:], 0.0)
         for v, vec in enumerate(vectors):
             nc.scalar.dma_start(out=bias_rows[v : v + 1, :], in_=vec.rearrange("(o h) -> o h", o=1))
+
+        warm_in = const.tile([P, 1], F32)
+        warm_out = const.tile([P, 1], F32)
+        nc.vector.memset(warm_in[:], 0.0)
+        nc.scalar.activation(out=warm_out[:], in_=warm_in[:], func=ACT.Gelu)
 
         def load_group(g):
             tiles = {}
@@ -90,12 +91,12 @@ def tile_cfccell_pa_t_kernel(
             return tiles
 
         def load_weight(name, w):
-            tile = const.tile([P, CHUNKS * H], BF16, name="rows_" + name)
+            w_rows = const.tile([P, CHUNKS * H], BF16, name="rows_" + name)
             nc.sync.dma_start(
-                out=tile[:].rearrange("r (u ek) -> r u ek", u=2),
+                out=w_rows[:].rearrange("r (u ek) -> r u ek", u=2),
                 in_=w.rearrange("(u r e) k -> r u (e k)", u=2, e=2),
             )
-            return tile
+            return w_rows
 
         live = {}
         weight_rows = {"ff2": load_weight("ff2", W_ff2)}
@@ -104,26 +105,31 @@ def tile_cfccell_pa_t_kernel(
             weight_rows[name] = load_weight(name, w)
         live[1] = {"rows": load_group(1)}
 
-        bias_planes = pools["psum_t"].tile([P, 2, P], F32, tag="transposed", name="bias_planes")
-        for u in range(2):
-            nc.tensor.transpose(
-                bias_planes[:, u, :], bias_rows[:].bitcast(F32)[:, u * P : (u + 1) * P], ident[:]
+        chunk_bias = {}
+
+        def spread_biases():
+            bias_planes = pools["psum_t"].tile([P, 2, P], F32, tag="transposed", name="bias_planes")
+            for u in range(2):
+                nc.tensor.transpose(
+                    bias_planes[:, u, :], bias_rows[:].bitcast(F32)[:, u * P : (u + 1) * P], ident[:]
+                )
+            bias = const.tile([P, len(vectors), CHUNKS], F32, name="bias")
+            nc.vector.tensor_copy(
+                out=bias[:].rearrange("p v (u e) -> p v u e", e=2),
+                in_=bias_planes[:].bitcast(BF16)[:, :, 0 : 2 * len(vectors)].rearrange(
+                    "p u (v e) -> p v u e", e=2
+                ),
             )
-        bias = const.tile([P, len(vectors), CHUNKS], F32)
-        nc.vector.tensor_copy(
-            out=bias[:].rearrange("p v (u e) -> p v u e", e=2),
-            in_=bias_planes[:].bitcast(BF16)[:, :, 0 : 2 * len(vectors)].rearrange(
-                "p u (v e) -> p v u e", e=2
-            ),
-        )
-        bias_ff2 = bias[:, 0, :]
-        bias_rec = bias[:, 5, :]
-        bias_in = const.tile([P, CHUNKS], F32)
-        nc.vector.tensor_tensor(out=bias_in[:], in0=bias[:, 3, :], in1=bias[:, 4, :], op=ALU.add)
-        bias_gate_sum = const.tile([P, CHUNKS], F32)
-        bias_gate = const.tile([P, CHUNKS], F32)
-        nc.vector.tensor_tensor(out=bias_gate_sum[:], in0=bias[:, 1, :], in1=bias[:, 2, :], op=ALU.add)
-        nc.vector.tensor_scalar_mul(out=bias_gate[:], in0=bias_gate_sum[:], scalar1=0.5)
+            chunk_bias["ff2"] = bias[:, 0, :]
+            chunk_bias["rec"] = bias[:, 5, :]
+            bias_in = const.tile([P, CHUNKS], F32, name="bias_in")
+            nc.vector.tensor_tensor(out=bias_in[:], in0=bias[:, 3, :], in1=bias[:, 4, :], op=ALU.add)
+            chunk_bias["in"] = bias_in[:]
+            bias_gate_sum = const.tile([P, CHUNKS], F32, name="bias_gate_sum")
+            bias_gate = const.tile([P, CHUNKS], F32, name="bias_gate")
+            nc.vector.tensor_tensor(out=bias_gate_sum[:], in0=bias[:, 1, :], in1=bias[:, 2, :], op=ALU.add)
+            nc.vector.tensor_scalar_mul(out=bias_gate[:], in0=bias_gate_sum[:], scalar1=0.5)
+            chunk_bias["gate"] = bias_gate[:]
 
         w_codes = {}
         w_scales = {}
@@ -136,13 +142,13 @@ def tile_cfccell_pa_t_kernel(
                 w_codes[name][:], w_scales[name][:], "grouped",
             )
 
-        def quantise_rows(name, rows, grouped_tag):
+        def prepare(name, g, grouped_tag):
             codes = pools["mx"].tile([P, GROUP], U32, align_bytes=64, tag="codes_" + name, name="codes_" + name)
             scales = pools["mx"].tile([P, GROUP], U8, align_bytes=64, tag="scales_" + name, name="scales_" + name)
             grouped = transpose_and_quantise(
-                nc, pools, rows[:], ident[:], nc.scalar.copy, codes[:], scales[:], grouped_tag
+                nc, pools, live[g]["rows"][name][:], ident[:], nc.scalar.copy, codes[:], scales[:], grouped_tag
             )
-            return codes, scales, grouped
+            live[g][name] = (codes, scales, grouped)
 
         def product(c, terms):
             acc = pools["psum_mx"].tile([P, GROUP], F32, tag="acc", name="acc")
@@ -158,26 +164,25 @@ def tile_cfccell_pa_t_kernel(
                 )
             return acc
 
-        out_groups = out.rearrange("(g p s) f -> g p s f", p=P, s=BLOCKS)
-
-
-        def prepare(name, g, grouped_tag):
-            live[g][name] = quantise_rows(name, live[g]["rows"][name], grouped_tag)
-
         def hidden_layer(g):
             codes, scales, grouped = live[g]["ff1"]
             ff2 = pools["work"].tile([P, CHUNKS, GROUP], BF16, name="ff2")
             for c in range(CHUNKS):
                 acc = product(c, [("ff2", codes, scales)])
-                nc.scalar.activation(out=ff2[:, c, :], in_=acc[:], func=ACT.Gelu, bias=bias_ff2[:, c : c + 1])
+                nc.scalar.activation(out=ff2[:, c, :], in_=acc[:], func=ACT.Gelu, bias=chunk_bias["ff2"][:, c : c + 1])
             ff2_grouped = pools["grouped"].tile([P, GROUP * PACK], BF16, align_bytes=64, name="ff2_grouped")
             nc.vector.tensor_copy(
                 out=ff2_grouped[:].rearrange("p (b i j) -> p b j i", i=4, j=PACK),
                 in_=ff2[:].rearrange("p j (b i) -> p b j i", i=4),
             )
+            live[g]["ff2_grouped"] = ff2_grouped
+
+        def quantise_hidden(g):
             ff2_codes = pools["mx"].tile([P, GROUP], U32, align_bytes=64, name="ff2_codes")
             ff2_scales = pools["mx"].tile([P, GROUP], U8, align_bytes=64, name="ff2_scales")
-            nc.vector.quantize_mx(out=ff2_codes[:].bitcast(FP8X4), scales=ff2_scales[:], in_=ff2_grouped[:])
+            nc.vector.quantize_mx(
+                out=ff2_codes[:].bitcast(FP8X4), scales=ff2_scales[:], in_=live[g]["ff2_grouped"][:]
+            )
             live[g]["ff2"] = (ff2_codes, ff2_scales)
 
         def input_part(g):
@@ -185,15 +190,12 @@ def tile_cfccell_pa_t_kernel(
             delta = pools["work"].tile([P, CHUNKS, GROUP], F32, name="delta")
             for c in range(CHUNKS):
                 acc = product(c, [("in", codes, scales)])
-                nc.scalar.activation(out=delta[:, c, :], in_=acc[:], func=ACT.Gelu, bias=bias_in[:, c : c + 1])
-            live[g]["delta"] = delta
-
-        def subtract_state(g):
-            delta = live[g]["delta"]
-            grouped = live[g]["hx"][2]
+                nc.scalar.activation(out=delta[:, c, :], in_=acc[:], func=ACT.Gelu, bias=chunk_bias["in"][:, c : c + 1])
+            hx_grouped = live[g]["hx"][2]
             nc.vector.tensor_tensor(
-                out=delta[:], in0=delta[:], in1=grouped[:].rearrange("p (b j) -> p j b", j=PACK), op=ALU.subtract
+                out=delta[:], in0=delta[:], in1=hx_grouped[:].rearrange("p (b j) -> p j b", j=PACK), op=ALU.subtract
             )
+            live[g]["delta"] = delta
 
         def recurrent_part(g):
             codes, scales, grouped = live[g]["hx"]
@@ -201,8 +203,8 @@ def tile_cfccell_pa_t_kernel(
             rec = pools["work"].tile([P, CHUNKS, GROUP], F32, name="rec")
             for c in range(CHUNKS):
                 acc = product(c, [("r", codes, scales)])
-                nc.scalar.activation(out=rec[:, c, :], in_=acc[:], func=ACT.Gelu, bias=bias_rec[:, c : c + 1])
-            for pair in (slice(0, 2), slice(2, 4)):
+                nc.scalar.activation(out=rec[:, c, :], in_=acc[:], func=ACT.Gelu, bias=chunk_bias["rec"][:, c : c + 1])
+            for pair in CHUNK_PAIRS:
                 nc.vector.tensor_tensor(out=delta[:, pair, :], in0=delta[:, pair, :], in1=rec[:, pair, :], op=ALU.add)
 
         def gate_part(g):
@@ -212,13 +214,15 @@ def tile_cfccell_pa_t_kernel(
             for c in range(CHUNKS):
                 acc = product(c, [("ta", codes, scales), ("tb", codes, scales)])
                 nc.scalar.activation(
-                    out=gate[:, c, :], in_=acc[:], func=ACT.Tanh, bias=bias_gate[:, c : c + 1], scale=0.5
+                    out=gate[:, c, :], in_=acc[:], func=ACT.Tanh, bias=chunk_bias["gate"][:, c : c + 1], scale=0.5
                 )
-            for pair in (slice(0, 2), slice(2, 4)):
+            for pair in CHUNK_PAIRS:
                 nc.vector.scalar_tensor_tensor(
                     out=delta[:, pair, :], in0=gate[:, pair, :], scalar=1.0, in1=delta[:, pair, :],
                     op0=ALU.add, op1=ALU.mult,
                 )
+
+        out_groups = out.rearrange("(g p s) f -> g p s f", p=P, s=BLOCKS)
 
         def blend_and_store(g):
             delta = live[g]["delta"]
@@ -243,6 +247,7 @@ def tile_cfccell_pa_t_kernel(
 
         prepare_weight("ff2")
         prepare("ff1", 0, "grouped")
+        spread_biases()
         prepare_weight("in")
         prepare("x", 0, "grouped")
         for name in ("r", "ta", "tb"):
@@ -252,8 +257,8 @@ def tile_cfccell_pa_t_kernel(
                 live[g + 2] = {"rows": load_group(g + 2)}
             hidden_layer(g)
             prepare("hx", g, "hx_grouped")
+            quantise_hidden(g)
             input_part(g)
-            subtract_state(g)
             if g + 1 < N_GROUPS:
                 prepare("ff1", g + 1, "grouped")
                 prepare("x", g + 1, "grouped")

@@ -69,41 +69,49 @@ def tile_cfccell_pa_t_kernel(
         ident = const.tile([P, P], F32)
         make_identity(nc, ident[:])
 
-        vectors = (b_ff2, b_ta, b_tb, b_in, input_b, r_b)
-        bias_rows = const.tile([P, H], BF16)
-        nc.vector.memset(bias_rows[:], 0.0)
-        for v, vec in enumerate(vectors):
-            nc.scalar.dma_start(out=bias_rows[v : v + 1, :], in_=vec.rearrange("(o h) -> o h", o=1))
-
         warm_in = const.tile([P, 1], F32)
         warm_out = const.tile([P, 1], F32)
         nc.vector.memset(warm_in[:], 0.0)
         nc.scalar.activation(out=warm_out[:], in_=warm_in[:], func=ACT.Gelu)
 
-        def load_group(g):
-            tiles = {}
-            for name, src in (("ff1", ff1), ("x", x), ("hx", hx)):
-                tiles[name] = pools["rows"].tile([P, BLOCKS * H], BF16, tag=name, name=name)
-                nc.sync.dma_start(
-                    out=tiles[name][:],
-                    in_=src.rearrange("(g p s) k -> g p (s k)", p=P, s=BLOCKS)[g],
-                )
-            return tiles
+        live = {g: {} for g in range(N_GROUPS)}
+        sources = {"ff1": ff1, "x": x, "hx": hx}
 
-        def load_weight(name, w):
+        def load_rows(name, g):
+            rows = pools["rows"].tile([P, BLOCKS * H], BF16, tag=name, name=name)
+            nc.sync.dma_start(
+                out=rows[:], in_=sources[name].rearrange("(g p s) k -> g p (s k)", p=P, s=BLOCKS)[g]
+            )
+            live[g]["rows_" + name] = rows
+
+        def load_group(g):
+            for name in ("ff1", "x", "hx"):
+                load_rows(name, g)
+
+        weights = {"ff2": W_ff2, "in": W_in, "r": W_r, "ta": W_ta, "tb": W_tb}
+        weight_rows = {}
+
+        def load_weight(name):
             w_rows = const.tile([P, CHUNKS * H], BF16, name="rows_" + name)
             nc.sync.dma_start(
                 out=w_rows[:].rearrange("r (u ek) -> r u ek", u=2),
-                in_=w.rearrange("(u r e) k -> r u (e k)", u=2, e=2),
+                in_=weights[name].rearrange("(u r e) k -> r u (e k)", u=2, e=2),
             )
-            return w_rows
+            weight_rows[name] = w_rows
 
-        live = {}
-        weight_rows = {"ff2": load_weight("ff2", W_ff2)}
-        live[0] = {"rows": load_group(0)}
-        for name, w in (("in", W_in), ("r", W_r), ("ta", W_ta), ("tb", W_tb)):
-            weight_rows[name] = load_weight(name, w)
-        live[1] = {"rows": load_group(1)}
+        load_weight("ff2")
+        load_rows("ff1", 0)
+        vectors = (b_ff2, b_ta, b_tb, b_in, input_b, r_b)
+        bias_rows = const.tile([P, H], BF16)
+        nc.vector.memset(bias_rows[:], 0.0)
+        for v, vec in enumerate(vectors):
+            nc.sync.dma_start(out=bias_rows[v : v + 1, :], in_=vec.rearrange("(o h) -> o h", o=1))
+        load_weight("in")
+        load_rows("x", 0)
+        for name in ("r", "ta", "tb"):
+            load_weight(name)
+        load_rows("hx", 0)
+        load_group(1)
 
         chunk_bias = {}
 
@@ -138,7 +146,7 @@ def tile_cfccell_pa_t_kernel(
             w_codes[name] = const.tile([P, H], U32, align_bytes=64, name="codes_" + name)
             w_scales[name] = const.tile([P, H], U8, align_bytes=64, name="scales_" + name)
             transpose_and_quantise(
-                nc, pools, weight_rows[name][:], ident[:], nc.vector.tensor_copy,
+                nc, pools, weight_rows[name][:], ident[:], nc.scalar.copy,
                 w_codes[name][:], w_scales[name][:], "grouped",
             )
 
@@ -146,7 +154,7 @@ def tile_cfccell_pa_t_kernel(
             codes = pools["mx"].tile([P, GROUP], U32, align_bytes=64, tag="codes_" + name, name="codes_" + name)
             scales = pools["mx"].tile([P, GROUP], U8, align_bytes=64, tag="scales_" + name, name="scales_" + name)
             grouped = transpose_and_quantise(
-                nc, pools, live[g]["rows"][name][:], ident[:], nc.scalar.copy, codes[:], scales[:], grouped_tag
+                nc, pools, live[g]["rows_" + name][:], ident[:], nc.scalar.copy, codes[:], scales[:], grouped_tag
             )
             live[g][name] = (codes, scales, grouped)
 
@@ -226,7 +234,7 @@ def tile_cfccell_pa_t_kernel(
 
         def blend_and_store(g):
             delta = live[g]["delta"]
-            hx_rows = live[g]["rows"]["hx"]
+            hx_rows = live[g]["rows_hx"]
             for s in range(BLOCKS):
                 back = pools["psum_t"].tile([P, H], F32, tag="transposed", name="back")
                 for c in range(CHUNKS):
@@ -254,7 +262,7 @@ def tile_cfccell_pa_t_kernel(
             prepare_weight(name)
         for g in range(N_GROUPS):
             if g + 2 < N_GROUPS:
-                live[g + 2] = {"rows": load_group(g + 2)}
+                load_group(g + 2)
             hidden_layer(g)
             prepare("hx", g, "hx_grouped")
             quantise_hidden(g)

@@ -20,32 +20,14 @@ BLOCKS = GROUP // P
 CHUNKS = H // P
 N_GROUPS = B // GROUP
 WORDS = H // 2
-CHUNK_PAIRS = (slice(0, 2), slice(2, 4))
+HALF = GROUP // 2
+
+FEATURE_BLOCKS = (0, 1)
+ROW_BLOCKS = (2, 3)
+FC = len(FEATURE_BLOCKS) * P
+PAIRS = (slice(0, 2), slice(2, 4))
 
 FLOPS = 5 * 2 * B * H * H
-
-
-def transpose_and_quantise(nc, pools, rows, ident, copy, codes, scales, grouped_tag):
-    words = rows.bitcast(F32)
-    grouped = pools["grouped"].tile([P, GROUP * PACK], BF16, align_bytes=64, tag=grouped_tag, name=grouped_tag)
-    grouped_words = grouped[:].bitcast(F32).rearrange("p (c u) -> p c u", u=2)
-    half_cols = GROUP // 2
-    for half in range(2):
-        planes = pools["psum_t"].tile([P, 2, half_cols], F32, tag="transposed", name="planes")
-        for s in range(2):
-            slot = 2 * half + s
-            for u in range(2):
-                nc.tensor.transpose(
-                    planes[:, u, s * P : (s + 1) * P],
-                    words[:, slot * WORDS + u * P : slot * WORDS + (u + 1) * P],
-                    ident,
-                )
-        copy(
-            out=grouped_words[:, half * half_cols : (half + 1) * half_cols, :],
-            in_=planes[:].rearrange("p u c -> p c u"),
-        )
-    nc.vector.quantize_mx(out=codes.bitcast(FP8X4), scales=scales, in_=grouped[:])
-    return grouped
 
 
 def tile_cfccell_pa_t_kernel(
@@ -53,225 +35,350 @@ def tile_cfccell_pa_t_kernel(
 ):
     nc = tc.nc
     with ExitStack() as stack:
-        pools = {
-            "const": stack.enter_context(tc.tile_pool(name="const", bufs=1)),
-            "rows": stack.enter_context(tc.tile_pool(name="rows", bufs=4)),
-            "grouped": stack.enter_context(tc.tile_pool(name="grouped", bufs=2)),
-            "mx": stack.enter_context(tc.tile_pool(name="mx", bufs=2)),
-            "work": stack.enter_context(tc.tile_pool(name="work", bufs=2)),
-            "store": stack.enter_context(tc.tile_pool(name="store", bufs=6)),
-            "psum_t": stack.enter_context(tc.psum_pool(name="psum_t", bufs=4)),
-            "psum_mx": stack.enter_context(tc.psum_pool(name="psum_mx", bufs=4)),
-        }
-        const = pools["const"]
+        const = stack.enter_context(tc.tile_pool(name="const", bufs=1))
+        rows_pool = stack.enter_context(tc.tile_pool(name="rows", bufs=4))
+        grouped_pool = stack.enter_context(tc.tile_pool(name="grouped", bufs=2))
+        mx = stack.enter_context(tc.tile_pool(name="mx", bufs=2))
+        work = stack.enter_context(tc.tile_pool(name="work", bufs=2))
+        store = stack.enter_context(tc.tile_pool(name="store", bufs=4))
+        psum_t = stack.enter_context(tc.psum_pool(name="psum_t", bufs=4))
+        psum_mx = stack.enter_context(tc.psum_pool(name="psum_mx", bufs=4))
         stack.enter_context(tc.manual_schedule())
 
-        ident = const.tile([P, P], F32)
+        ident = const.tile([P, P], F32, name="ident")
         make_identity(nc, ident[:])
-
-        warm_in = const.tile([P, 1], F32)
-        warm_out = const.tile([P, 1], F32)
+        warm_in = const.tile([P, 1], F32, name="warm_in")
+        warm_out = const.tile([P, 1], F32, name="warm_out")
         nc.vector.memset(warm_in[:], 0.0)
         nc.scalar.activation(out=warm_out[:], in_=warm_in[:], func=ACT.Gelu)
 
+        on_scalar = nc.scalar.copy
+        on_vector = nc.vector.tensor_copy
         live = {g: {} for g in range(N_GROUPS)}
         sources = {"ff1": ff1, "x": x, "hx": hx}
+        weights = {"ff2": W_ff2, "in": W_in, "r": W_r, "ta": W_ta, "tb": W_tb}
+        operands = {}
 
         def load_rows(name, g):
-            rows = pools["rows"].tile([P, BLOCKS * H], BF16, tag=name, name=name)
-            nc.sync.dma_start(
-                out=rows[:], in_=sources[name].rearrange("(g p s) k -> g p (s k)", p=P, s=BLOCKS)[g]
-            )
-            live[g]["rows_" + name] = rows
+            rows = rows_pool.tile([P, BLOCKS * H], BF16, tag=name, name=name)
+            nc.sync.dma_start(out=rows[:], in_=sources[name].rearrange("(g p s) k -> g p (s k)", p=P, s=BLOCKS)[g])
+            operands[name, g] = {"rows": rows}
 
         def load_group(g):
             for name in ("ff1", "x", "hx"):
                 load_rows(name, g)
 
-        weights = {"ff2": W_ff2, "in": W_in, "r": W_r, "ta": W_ta, "tb": W_tb}
-        weight_rows = {}
-
         def load_weight(name):
-            w_rows = const.tile([P, CHUNKS * H], BF16, name="rows_" + name)
+            rows = const.tile([P, CHUNKS * H], BF16, name="rows_" + name)
             nc.sync.dma_start(
-                out=w_rows[:].rearrange("r (u ek) -> r u ek", u=2),
+                out=rows[:].rearrange("r (u ek) -> r u ek", u=2),
                 in_=weights[name].rearrange("(u r e) k -> r u (e k)", u=2, e=2),
             )
-            weight_rows[name] = w_rows
+            operands[name, None] = {"rows": rows}
 
+        vectors = (b_ff2, b_ta, b_tb, b_in, input_b, r_b)
+        bias_rows = const.tile([P, H], BF16, name="bias_rows")
+        nc.vector.memset(bias_rows[:], 0.0)
         load_weight("ff2")
         load_rows("ff1", 0)
-        vectors = (b_ff2, b_ta, b_tb, b_in, input_b, r_b)
-        bias_rows = const.tile([P, H], BF16)
-        nc.vector.memset(bias_rows[:], 0.0)
         for v, vec in enumerate(vectors):
             nc.sync.dma_start(out=bias_rows[v : v + 1, :], in_=vec.rearrange("(o h) -> o h", o=1))
         load_weight("in")
         load_rows("x", 0)
-        for name in ("r", "ta", "tb"):
-            load_weight(name)
+        load_weight("r")
         load_rows("hx", 0)
+        load_weight("ta")
+        load_weight("tb")
         load_group(1)
 
         chunk_bias = {}
 
         def spread_biases():
-            bias_planes = pools["psum_t"].tile([P, 2, P], F32, tag="transposed", name="bias_planes")
+            bias_planes = psum_t.tile([P, 2, P], F32, tag="transposed", name="bias_planes")
             for u in range(2):
-                nc.tensor.transpose(
-                    bias_planes[:, u, :], bias_rows[:].bitcast(F32)[:, u * P : (u + 1) * P], ident[:]
-                )
+                nc.tensor.transpose(bias_planes[:, u, :], bias_rows[:].bitcast(F32)[:, u * P : (u + 1) * P], ident[:])
             bias = const.tile([P, len(vectors), CHUNKS], F32, name="bias")
             nc.vector.tensor_copy(
                 out=bias[:].rearrange("p v (u e) -> p v u e", e=2),
-                in_=bias_planes[:].bitcast(BF16)[:, :, 0 : 2 * len(vectors)].rearrange(
-                    "p u (v e) -> p v u e", e=2
-                ),
+                in_=bias_planes[:].bitcast(BF16)[:, :, 0 : 2 * len(vectors)].rearrange("p u (v e) -> p v u e", e=2),
             )
-            chunk_bias["ff2"] = bias[:, 0, :]
-            chunk_bias["rec"] = bias[:, 5, :]
+            chunk_bias["f"] = bias[:, 0, :]
+            chunk_bias["r"] = bias[:, 5, :]
             bias_in = const.tile([P, CHUNKS], F32, name="bias_in")
             nc.vector.tensor_tensor(out=bias_in[:], in0=bias[:, 3, :], in1=bias[:, 4, :], op=ALU.add)
-            chunk_bias["in"] = bias_in[:]
+            chunk_bias["i"] = bias_in[:]
             bias_gate_sum = const.tile([P, CHUNKS], F32, name="bias_gate_sum")
             bias_gate = const.tile([P, CHUNKS], F32, name="bias_gate")
             nc.vector.tensor_tensor(out=bias_gate_sum[:], in0=bias[:, 1, :], in1=bias[:, 2, :], op=ALU.add)
             nc.vector.tensor_scalar_mul(out=bias_gate[:], in0=bias_gate_sum[:], scalar1=0.5)
-            chunk_bias["gate"] = bias_gate[:]
+            chunk_bias["t"] = bias_gate[:]
 
-        w_codes = {}
-        w_scales = {}
+        def turn(name, g, half):
+            op = operands[name, g]
+            words = op["rows"][:].bitcast(F32)
+            planes = psum_t.tile([P, 2, HALF], F32, tag="transposed", name="planes")
+            for s in range(2):
+                slot = 2 * half + s
+                for u in range(2):
+                    nc.tensor.transpose(
+                        planes[:, u, s * P : (s + 1) * P],
+                        words[:, slot * WORDS + u * P : slot * WORDS + (u + 1) * P],
+                        ident[:],
+                    )
+            op["planes", half] = planes
 
-        def prepare_weight(name):
-            w_codes[name] = const.tile([P, H], U32, align_bytes=64, name="codes_" + name)
-            w_scales[name] = const.tile([P, H], U8, align_bytes=64, name="scales_" + name)
-            transpose_and_quantise(
-                nc, pools, weight_rows[name][:], ident[:], nc.scalar.copy,
-                w_codes[name][:], w_scales[name][:], "grouped",
-            )
-
-        def prepare(name, g, grouped_tag):
-            codes = pools["mx"].tile([P, GROUP], U32, align_bytes=64, tag="codes_" + name, name="codes_" + name)
-            scales = pools["mx"].tile([P, GROUP], U8, align_bytes=64, tag="scales_" + name, name="scales_" + name)
-            grouped = transpose_and_quantise(
-                nc, pools, live[g]["rows_" + name][:], ident[:], nc.scalar.copy, codes[:], scales[:], grouped_tag
-            )
-            live[g][name] = (codes, scales, grouped)
-
-        def product(c, terms):
-            acc = pools["psum_mx"].tile([P, GROUP], F32, tag="acc", name="acc")
-            for i, (weight, codes, scales) in enumerate(terms):
-                nc.tensor.matmul_mx(
-                    out=acc[:],
-                    lhsT=w_codes[weight][:, c * P : (c + 1) * P].bitcast(FP8X4),
-                    lhsT_scale=w_scales[weight][:, c * P : (c + 1) * P],
-                    rhs=codes[:].bitcast(FP8X4),
-                    rhs_scale=scales[:],
-                    start=(i == 0),
-                    stop=(i == len(terms) - 1),
+        def regroup(name, g, half, copy):
+            op = operands[name, g]
+            if half == 0:
+                tag = "hx_grouped" if name == "hx" else "grouped"
+                op["grouped"] = grouped_pool.tile(
+                    [P, GROUP * PACK], BF16, align_bytes=64, tag=tag, name=tag, bufs=2 if name == "hx" else 3
                 )
-            return acc
+            words = op["grouped"][:].bitcast(F32).rearrange("p (c u) -> p c u", u=2)
+            copy(
+                out=words[:, half * HALF : (half + 1) * HALF, :],
+                in_=op["planes", half][:].rearrange("p u c -> p c u"),
+            )
 
-        def hidden_layer(g):
-            codes, scales, grouped = live[g]["ff1"]
-            ff2 = pools["work"].tile([P, CHUNKS, GROUP], BF16, name="ff2")
-            for c in range(CHUNKS):
-                acc = product(c, [("ff2", codes, scales)])
-                nc.scalar.activation(out=ff2[:, c, :], in_=acc[:], func=ACT.Gelu, bias=chunk_bias["ff2"][:, c : c + 1])
-            ff2_grouped = pools["grouped"].tile([P, GROUP * PACK], BF16, align_bytes=64, name="ff2_grouped")
+        def quantise(name, g):
+            op = operands[name, g]
+            pool = const if g is None else mx
+            op["codes"] = pool.tile([P, GROUP], U32, align_bytes=64, tag="codes_" + name, name="codes_" + name)
+            op["scales"] = pool.tile([P, GROUP], U8, align_bytes=64, tag="scales_" + name, name="scales_" + name)
+            nc.vector.quantize_mx(out=op["codes"][:].bitcast(FP8X4), scales=op["scales"][:], in_=op["grouped"][:])
+
+        stages = {"f": ("ff1", ("ff2",)), "i": ("x", ("in",)), "r": ("hx", ("r",)), "t": ("h", ("ta", "tb"))}
+
+        def multiply(stage, g, chunks=range(CHUNKS)):
+            moving, names = stages[stage]
+            op = operands[moving, g]
+            for c in chunks:
+                acc = psum_mx.tile([P, GROUP], F32, tag="acc", name="acc")
+                for i, name in enumerate(names):
+                    w = operands[name, None]
+                    nc.tensor.matmul_mx(
+                        out=acc[:],
+                        lhsT=w["codes"][:, c * P : (c + 1) * P].bitcast(FP8X4),
+                        lhsT_scale=w["scales"][:, c * P : (c + 1) * P],
+                        rhs=op["codes"][:].bitcast(FP8X4),
+                        rhs_scale=op["scales"][:],
+                        start=(i == 0),
+                        stop=(i == len(names) - 1),
+                    )
+                live[g][stage, c] = acc
+
+        def activate(stage, g, chunks=range(CHUNKS)):
+            for c in chunks:
+                if c == 0:
+                    live[g][stage] = work.tile(
+                        [P, CHUNKS, GROUP], BF16 if stage == "f" else F32, tag="act_" + stage, name="act_" + stage
+                    )
+                nc.scalar.activation(
+                    out=live[g][stage][:, c, :],
+                    in_=live[g][stage, c][:],
+                    func=ACT.Tanh if stage == "t" else ACT.Gelu,
+                    bias=chunk_bias[stage][:, c : c + 1],
+                    scale=0.5 if stage == "t" else 1.0,
+                )
+
+        def interleave(g):
+            grouped = grouped_pool.tile([P, GROUP * PACK], BF16, align_bytes=64, tag="ff2_grouped", name="ff2_grouped", bufs=2)
             nc.vector.tensor_copy(
-                out=ff2_grouped[:].rearrange("p (b i j) -> p b j i", i=4, j=PACK),
-                in_=ff2[:].rearrange("p j (b i) -> p b j i", i=4),
+                out=grouped[:].rearrange("p (b i j) -> p b j i", i=4, j=PACK),
+                in_=live[g]["f"][:].rearrange("p j (b i) -> p b j i", i=4),
             )
-            live[g]["ff2_grouped"] = ff2_grouped
+            operands["h", g] = {"grouped": grouped}
 
-        def quantise_hidden(g):
-            ff2_codes = pools["mx"].tile([P, GROUP], U32, align_bytes=64, name="ff2_codes")
-            ff2_scales = pools["mx"].tile([P, GROUP], U8, align_bytes=64, name="ff2_scales")
-            nc.vector.quantize_mx(
-                out=ff2_codes[:].bitcast(FP8X4), scales=ff2_scales[:], in_=live[g]["ff2_grouped"][:]
-            )
-            live[g]["ff2"] = (ff2_codes, ff2_scales)
-
-        def input_part(g):
-            codes, scales, grouped = live[g]["x"]
-            delta = pools["work"].tile([P, CHUNKS, GROUP], F32, name="delta")
-            for c in range(CHUNKS):
-                acc = product(c, [("in", codes, scales)])
-                nc.scalar.activation(out=delta[:, c, :], in_=acc[:], func=ACT.Gelu, bias=chunk_bias["in"][:, c : c + 1])
-            hx_grouped = live[g]["hx"][2]
+        def subtract(g):
+            delta = work.tile([P, CHUNKS, FC], F32, name="delta")
+            grouped = operands["hx", g]["grouped"]
             nc.vector.tensor_tensor(
-                out=delta[:], in0=delta[:], in1=hx_grouped[:].rearrange("p (b j) -> p j b", j=PACK), op=ALU.subtract
+                out=delta[:],
+                in0=live[g]["i"][:, :, 0:FC],
+                in1=grouped[:, 0 : FC * PACK].rearrange("p (b j) -> p j b", j=PACK),
+                op=ALU.subtract,
             )
             live[g]["delta"] = delta
 
-        def recurrent_part(g):
-            codes, scales, grouped = live[g]["hx"]
+        def add(g, pair):
             delta = live[g]["delta"]
-            rec = pools["work"].tile([P, CHUNKS, GROUP], F32, name="rec")
-            for c in range(CHUNKS):
-                acc = product(c, [("r", codes, scales)])
-                nc.scalar.activation(out=rec[:, c, :], in_=acc[:], func=ACT.Gelu, bias=chunk_bias["rec"][:, c : c + 1])
-            for pair in CHUNK_PAIRS:
-                nc.vector.tensor_tensor(out=delta[:, pair, :], in0=delta[:, pair, :], in1=rec[:, pair, :], op=ALU.add)
+            nc.vector.tensor_tensor(out=delta[:, pair, :], in0=delta[:, pair, :], in1=live[g]["r"][:, pair, 0:FC], op=ALU.add)
 
-        def gate_part(g):
-            codes, scales = live[g]["ff2"]
+        def gate(g, pair):
             delta = live[g]["delta"]
-            gate = pools["work"].tile([P, CHUNKS, GROUP], F32, name="gate")
-            for c in range(CHUNKS):
-                acc = product(c, [("ta", codes, scales), ("tb", codes, scales)])
-                nc.scalar.activation(
-                    out=gate[:, c, :], in_=acc[:], func=ACT.Tanh, bias=chunk_bias["gate"][:, c : c + 1], scale=0.5
-                )
-            for pair in CHUNK_PAIRS:
-                nc.vector.scalar_tensor_tensor(
-                    out=delta[:, pair, :], in0=gate[:, pair, :], scalar=1.0, in1=delta[:, pair, :],
-                    op0=ALU.add, op1=ALU.mult,
-                )
+            nc.vector.scalar_tensor_tensor(
+                out=delta[:, pair, :], in0=live[g]["t"][:, pair, 0:FC], scalar=1.0, in1=delta[:, pair, :],
+                op0=ALU.add, op1=ALU.mult,
+            )
 
         out_groups = out.rearrange("(g p s) f -> g p s f", p=P, s=BLOCKS)
 
-        def blend_and_store(g):
-            delta = live[g]["delta"]
-            hx_rows = live[g]["rows_hx"]
-            for s in range(BLOCKS):
-                back = pools["psum_t"].tile([P, H], F32, tag="transposed", name="back")
-                for c in range(CHUNKS):
-                    u, e = divmod(c, 2)
-                    nc.tensor.transpose(
-                        back[:, e * WORDS + u * P : e * WORDS + (u + 1) * P], delta[:, c, s * P : (s + 1) * P], ident[:]
-                    )
-                result = pools["store"].tile([P, H], F32, name="result")
-                nc.vector.scalar_tensor_tensor(
-                    out=result[:].rearrange("b (q e) -> b q e", e=2),
-                    in0=back[:].rearrange("b (e q) -> b q e", e=2),
-                    scalar=0.5,
-                    in1=hx_rows[:, s * H : (s + 1) * H].rearrange("b (q e) -> b q e", e=2),
-                    op0=ALU.mult,
-                    op1=ALU.add,
-                )
-                nc.sync.dma_start(out=out_groups[g][:, s, :], in_=result[:])
+        def pairs_of(ap):
+            return ap.rearrange("b (q e) -> b q e", e=2)
 
-        prepare_weight("ff2")
-        prepare("ff1", 0, "grouped")
+        def hx_block(g, s):
+            return operands["hx", g]["rows"][:, s * H : (s + 1) * H]
+
+        def turn_back(g, s, terms, key):
+            bank = psum_t.tile([P, H], F32, tag="transposed", name=key)
+            for c in range(CHUNKS):
+                u, e = divmod(c, 2)
+                for i, term in enumerate(terms):
+                    nc.tensor.matmul(
+                        bank[:, e * WORDS + u * P : e * WORDS + (u + 1) * P],
+                        lhsT=term[:, c, s * P : (s + 1) * P],
+                        rhs=ident[:],
+                        is_transpose=True,
+                        start=(i == 0),
+                        stop=(i == len(terms) - 1),
+                    )
+            live[g][key, s] = bank
+
+        def from_bank(g, key, s):
+            return live[g][key, s][:].rearrange("b (e q) -> b q e", e=2)
+
+        def B_(g, s):
+            turn_back(g, s, [live[g]["delta"]], "back")
+
+        def E_(g, s):
+            result = store.tile([P, H], F32, name="result")
+            nc.vector.scalar_tensor_tensor(
+                out=pairs_of(result[:]), in0=from_bank(g, "back", s), scalar=0.5, in1=pairs_of(hx_block(g, s)),
+                op0=ALU.mult, op1=ALU.add,
+            )
+            nc.sync.dma_start(out=out_groups[g][:, s, :], in_=result[:])
+
+        def V_(g, s):
+            turn_back(g, s, [live[g]["i"], live[g]["r"]], "sum")
+
+        def U_(g, s):
+            u = store.tile([P, H], F32, name="u")
+            nc.vector.tensor_tensor(out=pairs_of(u[:]), in0=from_bank(g, "sum", s), in1=pairs_of(hx_block(g, s)), op=ALU.subtract)
+            live[g]["u", s] = u
+
+        def H_(g, s):
+            turn_back(g, s, [live[g]["t"]], "gate")
+
+        def W_(g, s):
+            w = store.tile([P, H], F32, name="w")
+            nc.vector.scalar_tensor_tensor(
+                out=pairs_of(w[:]), in0=from_bank(g, "gate", s), scalar=1.0, in1=pairs_of(live[g]["u", s][:]),
+                op0=ALU.add, op1=ALU.mult,
+            )
+            live[g]["w", s] = w
+
+        def Z_(g, s):
+            result = store.tile([P, H], F32, name="result")
+            nc.vector.scalar_tensor_tensor(
+                out=result[:], in0=live[g]["w", s][:], scalar=0.5, in1=hx_block(g, s), op0=ALU.mult, op1=ALU.add
+            )
+            nc.sync.dma_start(out=out_groups[g][:, s, :], in_=result[:])
+
+        turn("ff2", None, 0); turn("ff2", None, 1)
+        turn("ff1", 0, 0); turn("ff1", 0, 1)
+        regroup("ff2", None, 0, on_scalar); regroup("ff2", None, 1, on_vector)
+        regroup("ff1", 0, 0, on_scalar); regroup("ff1", 0, 1, on_vector)
+        quantise("ff2", None); quantise("ff1", 0)
         spread_biases()
-        prepare_weight("in")
-        prepare("x", 0, "grouped")
-        for name in ("r", "ta", "tb"):
-            prepare_weight(name)
+        turn("in", None, 0); turn("in", None, 1); turn("x", 0, 0)
+        regroup("in", None, 0, on_scalar)
+        multiply("f", 0)
+        regroup("in", None, 1, on_vector)
+        turn("x", 0, 1)
+        regroup("x", 0, 0, on_scalar)
+        regroup("x", 0, 1, on_vector)
+        quantise("in", None)
+        activate("f", 0, (0, 1))
+        quantise("x", 0)
+        activate("f", 0, (2, 3))
+        turn("r", None, 0); turn("r", None, 1); turn("hx", 0, 0); turn("hx", 0, 1)
+        multiply("i", 0)
+        regroup("r", None, 0, on_vector); regroup("r", None, 1, on_vector)
+        quantise("r", None)
+        regroup("hx", 0, 0, on_scalar)
+        regroup("hx", 0, 1, on_vector)
+        interleave(0)
+        activate("i", 0)
+        turn("ta", None, 0); turn("ta", None, 1)
+        quantise("hx", 0)
+        quantise("h", 0)
+        regroup("ta", None, 0, on_scalar); regroup("ta", None, 1, on_vector)
+        turn("tb", None, 0); turn("tb", None, 1)
+        quantise("ta", None)
+        multiply("r", 0)
+        regroup("tb", None, 0, on_scalar); regroup("tb", None, 1, on_vector)
+        quantise("tb", None)
+        subtract(0)
         for g in range(N_GROUPS):
+            n = g + 1
+            last = n == N_GROUPS
             if g + 2 < N_GROUPS:
                 load_group(g + 2)
-            hidden_layer(g)
-            prepare("hx", g, "hx_grouped")
-            quantise_hidden(g)
-            input_part(g)
-            if g + 1 < N_GROUPS:
-                prepare("ff1", g + 1, "grouped")
-                prepare("x", g + 1, "grouped")
-            recurrent_part(g)
             if g > 0:
-                blend_and_store(g - 1)
-            gate_part(g)
-        blend_and_store(N_GROUPS - 1)
+                multiply("f", g, (0, 1, 2))
+                turn("hx", g, 0); turn("hx", g, 1)
+                activate("f", g, (0, 1, 2)); regroup("hx", g, 0, on_scalar)
+                gate(g - 1, PAIRS[0])
+                for s in ROW_BLOCKS[:1]: U_(g - 1, s)
+                gate(g - 1, PAIRS[1])
+                regroup("hx", g, 1, on_vector)
+                for s in ROW_BLOCKS[:1]: H_(g - 1, s)
+                for s in ROW_BLOCKS[1:]: V_(g - 1, s)
+                multiply("f", g, (3,)); activate("f", g, (3,))
+                for s in ROW_BLOCKS[:1]: W_(g - 1, s)
+                for s in ROW_BLOCKS[1:]: U_(g - 1, s)
+                multiply("i", g, (0, 1, 2))
+                for s in FEATURE_BLOCKS[:1]: B_(g - 1, s)
+                quantise("hx", g); interleave(g)
+                activate("i", g, (0, 1, 2))
+                multiply("r", g, (0,))
+            if not last:
+                turn("ff1", n, 0)
+            if g > 0:
+                multiply("i", g, (3,))
+                activate("r", g, (0,))
+                for s in FEATURE_BLOCKS[1:]: B_(g - 1, s)
+                for s in FEATURE_BLOCKS[:1]: E_(g - 1, s)
+                quantise("h", g)
+                for s in FEATURE_BLOCKS[1:]: E_(g - 1, s)
+                multiply("r", g, (1,))
+            if not last:
+                regroup("ff1", n, 0, on_scalar)
+                turn("ff1", n, 1); turn("x", n, 0)
+            if g > 0:
+                activate("i", g, (3,))
+                subtract(g)
+                for s in ROW_BLOCKS[1:]: H_(g - 1, s)
+                for s in ROW_BLOCKS[1:]: W_(g - 1, s)
+                for s in ROW_BLOCKS[:1]: Z_(g - 1, s)
+                multiply("r", g, (2, 3))
+                activate("r", g, (1,))
+            else:
+                activate("r", g, (0, 1))
+            if not last:
+                regroup("ff1", n, 1, on_scalar)
+            add(g, PAIRS[0])
+            activate("r", g, (2, 3))
+            add(g, PAIRS[1])
+            if g > 0:
+                for s in ROW_BLOCKS[1:]: Z_(g - 1, s)
+            multiply("t", g, (0, 1))
+            if not last:
+                quantise("ff1", n)
+                turn("x", n, 1)
+            activate("t", g, (0,))
+            if not last:
+                regroup("x", n, 0, on_scalar); regroup("x", n, 1, on_scalar)
+                quantise("x", n)
+            activate("t", g, (1,))
+            multiply("t", g, (2,))
+            for s in ROW_BLOCKS[:1]: V_(g, s)
+            multiply("t", g, (3,))
+            activate("t", g, (2, 3))
+        g = N_GROUPS - 1
+        gate(g, PAIRS[0]); gate(g, PAIRS[1])
+        for s in ROW_BLOCKS[1:]: V_(g, s)
+        for s in ROW_BLOCKS: U_(g, s)
+        for s in FEATURE_BLOCKS: B_(g, s)
+        for s in ROW_BLOCKS: H_(g, s); W_(g, s); Z_(g, s)
+        for s in FEATURE_BLOCKS: E_(g, s)

@@ -22,8 +22,8 @@ N_GROUPS = B // GROUP
 WORDS = H // 2
 HALF = GROUP // 2
 
-FEATURE_BLOCKS = (0, 1)
-ROW_BLOCKS = (2, 3)
+FEATURE_BLOCKS = (0, 1, 2, 3)
+ROW_BLOCKS = ()
 FC = len(FEATURE_BLOCKS) * P
 PAIRS = (slice(0, 2), slice(2, 4))
 
@@ -59,30 +59,38 @@ def tile_cfccell_pa_t_kernel(
         weights = {"ff2": W_ff2, "in": W_in, "r": W_r, "ta": W_ta, "tb": W_tb}
         operands = {}
 
-        def load_rows(name, g):
+        def load_rows(name, g, pieces=1):
             rows = rows_pool.tile([P, BLOCKS * H], BF16, tag=name, name=name)
-            nc.sync.dma_start(out=rows[:], in_=sources[name].rearrange("(g p s) k -> g p (s k)", p=P, s=BLOCKS)[g])
+            run = BLOCKS * H // pieces
+            for i in range(pieces):
+                nc.sync.dma_start(
+                    out=rows[:, i * run : (i + 1) * run],
+                    in_=sources[name].rearrange("(g p s) k -> g p (s k)", p=P, s=BLOCKS)[g][:, i * run : (i + 1) * run],
+                )
             operands[name, g] = {"rows": rows}
 
         def load_group(g):
             for name in ("ff1", "x", "hx"):
                 load_rows(name, g)
 
-        def load_weight(name):
+        def load_weight(name, pieces=1):
             rows = const.tile([P, CHUNKS * H], BF16, name="rows_" + name)
-            nc.sync.dma_start(
-                out=rows[:].rearrange("r (u ek) -> r u ek", u=2),
-                in_=weights[name].rearrange("(u r e) k -> r u (e k)", u=2, e=2),
-            )
+            step = 2 // pieces
+            for i in range(pieces):
+                u = slice(i * step, (i + 1) * step)
+                nc.sync.dma_start(
+                    out=rows[:].rearrange("r (u ek) -> r u ek", u=2)[:, u, :],
+                    in_=weights[name].rearrange("(u r e) k -> r u (e k)", u=2, e=2)[:, u, :],
+                )
             operands[name, None] = {"rows": rows}
 
         vectors = (b_ff2, b_ta, b_tb, b_in, input_b, r_b)
         bias_rows = const.tile([P, H], BF16, name="bias_rows")
         nc.vector.memset(bias_rows[:], 0.0)
-        load_weight("ff2")
-        load_rows("ff1", 0)
         for v, vec in enumerate(vectors):
-            nc.sync.dma_start(out=bias_rows[v : v + 1, :], in_=vec.rearrange("(o h) -> o h", o=1))
+            nc.scalar.dma_start(out=bias_rows[v : v + 1, :], in_=vec.rearrange("(o h) -> o h", o=1))
+        load_weight("ff2", 2)
+        load_rows("ff1", 0, 2)
         load_weight("in")
         load_rows("x", 0)
         load_weight("r")
@@ -129,7 +137,7 @@ def tile_cfccell_pa_t_kernel(
 
         def regroup(name, g, half, copy):
             op = operands[name, g]
-            if half == 0:
+            if "grouped" not in op:
                 tag = "hx_grouped" if name == "hx" else "grouped"
                 op["grouped"] = grouped_pool.tile(
                     [P, GROUP * PACK], BF16, align_bytes=64, tag=tag, name=tag, bufs=2 if name == "hx" else 3
@@ -189,20 +197,21 @@ def tile_cfccell_pa_t_kernel(
             )
             operands["h", g] = {"grouped": grouped}
 
-        def subtract(g):
-            delta = work.tile([P, CHUNKS, FC], F32, name="delta")
+        def subtract(g, pair):
+            if pair == PAIRS[0]:
+                live[g]["delta"] = work.tile([P, CHUNKS, FC], F32, name="delta", bufs=3)
+            delta = live[g]["delta"]
             grouped = operands["hx", g]["grouped"]
             nc.vector.tensor_tensor(
-                out=delta[:],
-                in0=live[g]["i"][:, :, 0:FC],
-                in1=grouped[:, 0 : FC * PACK].rearrange("p (b j) -> p j b", j=PACK),
+                out=delta[:, pair, :],
+                in0=live[g]["i"][:, pair, 0:FC],
+                in1=grouped[:, 0 : FC * PACK].rearrange("p (b j) -> p j b", j=PACK)[:, pair, :],
                 op=ALU.subtract,
             )
-            live[g]["delta"] = delta
 
-        def add(g, pair):
+        def add(g, chunks, engine):
             delta = live[g]["delta"]
-            nc.vector.tensor_tensor(out=delta[:, pair, :], in0=delta[:, pair, :], in1=live[g]["r"][:, pair, 0:FC], op=ALU.add)
+            engine.tensor_tensor(out=delta[:, chunks, :], in0=delta[:, chunks, :], in1=live[g]["r"][:, chunks, 0:FC], op=ALU.add)
 
         def gate(g, pair):
             delta = live[g]["delta"]
@@ -275,110 +284,68 @@ def tile_cfccell_pa_t_kernel(
             nc.sync.dma_start(out=out_groups[g][:, s, :], in_=result[:])
 
         turn("ff2", None, 0); turn("ff2", None, 1)
-        turn("ff1", 0, 0); turn("ff1", 0, 1)
         regroup("ff2", None, 0, on_scalar); regroup("ff2", None, 1, on_vector)
-        regroup("ff1", 0, 0, on_scalar); regroup("ff1", 0, 1, on_vector)
-        quantise("ff2", None); quantise("ff1", 0)
         spread_biases()
-        turn("in", None, 0); turn("in", None, 1); turn("x", 0, 0)
-        regroup("in", None, 0, on_scalar)
+        turn("ff1", 0, 0); turn("ff1", 0, 1)
+        regroup("ff1", 0, 0, on_scalar); regroup("ff1", 0, 1, on_vector)
+        quantise("ff2", None)
+        quantise("ff1", 0)
+        turn("in", None, 0); turn("in", None, 1)
+        regroup("in", None, 0, on_scalar); regroup("in", None, 1, on_vector)
+        turn("x", 0, 0); turn("x", 0, 1)
         multiply("f", 0)
-        regroup("in", None, 1, on_vector)
-        turn("x", 0, 1)
         regroup("x", 0, 0, on_scalar)
-        regroup("x", 0, 1, on_vector)
         quantise("in", None)
-        activate("f", 0, (0, 1))
+        regroup("x", 0, 1, on_vector)
+        activate("f", 0)
         quantise("x", 0)
-        activate("f", 0, (2, 3))
         turn("r", None, 0); turn("r", None, 1); turn("hx", 0, 0); turn("hx", 0, 1)
         multiply("i", 0)
         regroup("r", None, 0, on_vector); regroup("r", None, 1, on_vector)
-        quantise("r", None)
-        regroup("hx", 0, 0, on_scalar)
-        regroup("hx", 0, 1, on_vector)
-        interleave(0)
+        regroup("hx", 0, 0, on_scalar); regroup("hx", 0, 1, on_vector)
         activate("i", 0)
-        turn("ta", None, 0); turn("ta", None, 1)
+        interleave(0)
+        quantise("r", None)
         quantise("hx", 0)
+        turn("ta", None, 0); turn("ta", None, 1); turn("tb", None, 0); turn("tb", None, 1)
+        regroup("ta", None, 0, on_scalar); regroup("ta", None, 1, on_scalar)
         quantise("h", 0)
-        regroup("ta", None, 0, on_scalar); regroup("ta", None, 1, on_vector)
-        turn("tb", None, 0); turn("tb", None, 1)
-        quantise("ta", None)
-        multiply("r", 0)
         regroup("tb", None, 0, on_scalar); regroup("tb", None, 1, on_vector)
-        quantise("tb", None)
-        subtract(0)
+        quantise("ta", None); quantise("tb", None)
         for g in range(N_GROUPS):
             n = g + 1
             last = n == N_GROUPS
             if g + 2 < N_GROUPS:
                 load_group(g + 2)
             if g > 0:
-                multiply("f", g, (0, 1, 2))
+                multiply("f", g, (0, 1))
                 turn("hx", g, 0); turn("hx", g, 1)
-                activate("f", g, (0, 1, 2)); regroup("hx", g, 0, on_scalar)
-                gate(g - 1, PAIRS[0])
-                for s in ROW_BLOCKS[:1]: U_(g - 1, s)
-                gate(g - 1, PAIRS[1])
+                multiply("f", g, (2, 3))
+                activate("f", g)
                 regroup("hx", g, 1, on_vector)
-                for s in ROW_BLOCKS[:1]: H_(g - 1, s)
-                for s in ROW_BLOCKS[1:]: V_(g - 1, s)
-                multiply("f", g, (3,)); activate("f", g, (3,))
-                for s in ROW_BLOCKS[:1]: W_(g - 1, s)
-                for s in ROW_BLOCKS[1:]: U_(g - 1, s)
-                multiply("i", g, (0, 1, 2))
-                for s in FEATURE_BLOCKS[:1]: B_(g - 1, s)
-                quantise("hx", g); interleave(g)
-                activate("i", g, (0, 1, 2))
-                multiply("r", g, (0,))
-            if not last:
-                turn("ff1", n, 0)
-            if g > 0:
-                multiply("i", g, (3,))
-                activate("r", g, (0,))
-                for s in FEATURE_BLOCKS[1:]: B_(g - 1, s)
-                for s in FEATURE_BLOCKS[:1]: E_(g - 1, s)
+                regroup("hx", g, 0, on_scalar)
+                gate(g - 1, PAIRS[0]); gate(g - 1, PAIRS[1])
+                interleave(g)
+                quantise("hx", g)
                 quantise("h", g)
-                for s in FEATURE_BLOCKS[1:]: E_(g - 1, s)
-                multiply("r", g, (1,))
+                multiply("i", g)
+                activate("i", g)
+            subtract(g, PAIRS[0])
             if not last:
-                regroup("ff1", n, 0, on_scalar)
-                turn("ff1", n, 1); turn("x", n, 0)
-            if g > 0:
-                activate("i", g, (3,))
-                subtract(g)
-                for s in ROW_BLOCKS[1:]: H_(g - 1, s)
-                for s in ROW_BLOCKS[1:]: W_(g - 1, s)
-                for s in ROW_BLOCKS[:1]: Z_(g - 1, s)
-                multiply("r", g, (2, 3))
-                activate("r", g, (1,))
-            else:
-                activate("r", g, (0, 1))
-            if not last:
-                regroup("ff1", n, 1, on_scalar)
-            add(g, PAIRS[0])
-            activate("r", g, (2, 3))
-            add(g, PAIRS[1])
-            if g > 0:
-                for s in ROW_BLOCKS[1:]: Z_(g - 1, s)
-            multiply("t", g, (0, 1))
-            if not last:
-                quantise("ff1", n)
-                turn("x", n, 1)
-            activate("t", g, (0,))
-            if not last:
+                turn("ff1", n, 0); turn("ff1", n, 1); turn("x", n, 0); turn("x", n, 1)
+                regroup("ff1", n, 0, on_scalar); regroup("ff1", n, 1, on_scalar)
                 regroup("x", n, 0, on_scalar); regroup("x", n, 1, on_scalar)
+                quantise("ff1", n)
                 quantise("x", n)
-            activate("t", g, (1,))
-            multiply("t", g, (2,))
-            for s in ROW_BLOCKS[:1]: V_(g, s)
-            multiply("t", g, (3,))
-            activate("t", g, (2, 3))
+            multiply("r", g)
+            activate("r", g)
+            add(g, PAIRS[0], nc.vector)
+            subtract(g, PAIRS[1])
+            add(g, slice(2, 3), nc.gpsimd); add(g, slice(3, 4), nc.gpsimd)
+            if g > 0:
+                for s in FEATURE_BLOCKS: B_(g - 1, s); E_(g - 1, s)
+            multiply("t", g)
+            activate("t", g)
         g = N_GROUPS - 1
         gate(g, PAIRS[0]); gate(g, PAIRS[1])
-        for s in ROW_BLOCKS[1:]: V_(g, s)
-        for s in ROW_BLOCKS: U_(g, s)
-        for s in FEATURE_BLOCKS: B_(g, s)
-        for s in ROW_BLOCKS: H_(g, s); W_(g, s); Z_(g, s)
-        for s in FEATURE_BLOCKS: E_(g, s)
+        for s in FEATURE_BLOCKS: B_(g, s); E_(g, s)

@@ -22,9 +22,7 @@ N_GROUPS = B // GROUP
 WORDS = H // 2
 HALF = GROUP // 2
 
-FEATURE_BLOCKS = (0, 1, 2, 3)
-ROW_BLOCKS = ()
-FC = len(FEATURE_BLOCKS) * P
+ROW_COUNT = (0, 0, 0, 0, 0, 0, 0, 0)
 PAIRS = (slice(0, 2), slice(2, 4))
 
 FLOPS = 5 * 2 * B * H * H
@@ -40,13 +38,15 @@ def tile_cfccell_pa_t_kernel(
         grouped_pool = stack.enter_context(tc.tile_pool(name="grouped", bufs=2))
         mx = stack.enter_context(tc.tile_pool(name="mx", bufs=2))
         work = stack.enter_context(tc.tile_pool(name="work", bufs=2))
-        store = stack.enter_context(tc.tile_pool(name="store", bufs=4))
+        store = stack.enter_context(tc.tile_pool(name="store", bufs=6))
         psum_t = stack.enter_context(tc.psum_pool(name="psum_t", bufs=4))
         psum_mx = stack.enter_context(tc.psum_pool(name="psum_mx", bufs=4))
         stack.enter_context(tc.manual_schedule())
 
         ident = const.tile([P, P], F32, name="ident")
         make_identity(nc, ident[:])
+        twice = const.tile([P, P], BF16, name="twice")
+        nc.vector.tensor_scalar_mul(out=twice[:], in0=ident[:], scalar1=2.0)
         warm_in = const.tile([P, 1], F32, name="warm_in")
         warm_out = const.tile([P, 1], F32, name="warm_out")
         nc.vector.memset(warm_in[:], 0.0)
@@ -87,10 +87,10 @@ def tile_cfccell_pa_t_kernel(
         vectors = (b_ff2, b_ta, b_tb, b_in, input_b, r_b)
         bias_rows = const.tile([P, H], BF16, name="bias_rows")
         nc.vector.memset(bias_rows[:], 0.0)
-        for v, vec in enumerate(vectors):
-            nc.scalar.dma_start(out=bias_rows[v : v + 1, :], in_=vec.rearrange("(o h) -> o h", o=1))
         load_weight("ff2", 2)
         load_rows("ff1", 0, 2)
+        for v, vec in enumerate(vectors):
+            nc.sync.dma_start(out=bias_rows[v : v + 1, :], in_=vec.rearrange("(o h) -> o h", o=1))
         load_weight("in")
         load_rows("x", 0)
         load_weight("r")
@@ -197,9 +197,19 @@ def tile_cfccell_pa_t_kernel(
             )
             operands["h", g] = {"grouped": grouped}
 
+        def row_blocks(g):
+            return range(BLOCKS - ROW_COUNT[g], BLOCKS)
+
+        def feature_blocks(g):
+            return range(BLOCKS - ROW_COUNT[g])
+
+        def cols_of(g):
+            return slice(0, (BLOCKS - ROW_COUNT[g]) * P)
+
         def subtract(g, pair):
+            FC = cols_of(g).stop
             if pair == PAIRS[0]:
-                live[g]["delta"] = work.tile([P, CHUNKS, FC], F32, name="delta", bufs=3)
+                live[g]["delta"] = work.tile([P, CHUNKS, FC], F32, name="delta%d" % FC, bufs=2)
             delta = live[g]["delta"]
             grouped = operands["hx", g]["grouped"]
             nc.vector.tensor_tensor(
@@ -210,10 +220,12 @@ def tile_cfccell_pa_t_kernel(
             )
 
         def add(g, chunks, engine):
+            FC = cols_of(g).stop
             delta = live[g]["delta"]
             engine.tensor_tensor(out=delta[:, chunks, :], in0=delta[:, chunks, :], in1=live[g]["r"][:, chunks, 0:FC], op=ALU.add)
 
         def gate(g, pair):
+            FC = cols_of(g).stop
             delta = live[g]["delta"]
             nc.vector.scalar_tensor_tensor(
                 out=delta[:, pair, :], in0=live[g]["t"][:, pair, 0:FC], scalar=1.0, in1=delta[:, pair, :],
@@ -257,11 +269,41 @@ def tile_cfccell_pa_t_kernel(
             )
             nc.sync.dma_start(out=out_groups[g][:, s, :], in_=result[:])
 
+        def gate_cols(g, half):
+            delta = live[g]["delta"]
+            cols = slice(half * HALF, (half + 1) * HALF)
+            nc.vector.scalar_tensor_tensor(
+                out=delta[:, :, cols], in0=live[g]["t"][:, :, cols], scalar=1.0, in1=delta[:, :, cols],
+                op0=ALU.add, op1=ALU.mult,
+            )
+
+        def BX_(g, s):
+            bank = psum_t.tile([P, H], F32, tag="transposed", name="back")
+            nc.tensor.matmul(
+                bank[:], lhsT=twice[:], rhs=hx_block(g, s).rearrange("b (q e) -> b e q", e=2), start=True, stop=False
+            )
+            for c in range(CHUNKS):
+                u, e = divmod(c, 2)
+                nc.tensor.matmul(
+                    bank[:, e * WORDS + u * P : e * WORDS + (u + 1) * P],
+                    lhsT=live[g]["delta"][:, c, s * P : (s + 1) * P],
+                    rhs=ident[:],
+                    is_transpose=True,
+                    start=False,
+                    stop=(c == CHUNKS - 1),
+                )
+            live[g]["back", s] = bank
+
+        def EA_(g, s):
+            result = store.tile([P, H], F32, name="result")
+            nc.scalar.activation(out=pairs_of(result[:]), in_=from_bank(g, "back", s), func=ACT.Copy, scale=0.5)
+            nc.sync.dma_start(out=out_groups[g][:, s, :], in_=result[:])
+
         def V_(g, s):
             turn_back(g, s, [live[g]["i"], live[g]["r"]], "sum")
 
         def U_(g, s):
-            u = store.tile([P, H], F32, name="u")
+            u = store.tile([P, H], F32, name="u", bufs=3)
             nc.vector.tensor_tensor(out=pairs_of(u[:]), in0=from_bank(g, "sum", s), in1=pairs_of(hx_block(g, s)), op=ALU.subtract)
             live[g]["u", s] = u
 
@@ -269,7 +311,7 @@ def tile_cfccell_pa_t_kernel(
             turn_back(g, s, [live[g]["t"]], "gate")
 
         def W_(g, s):
-            w = store.tile([P, H], F32, name="w")
+            w = store.tile([P, H], F32, name="w", bufs=2)
             nc.vector.scalar_tensor_tensor(
                 out=pairs_of(w[:]), in0=from_bank(g, "gate", s), scalar=1.0, in1=pairs_of(live[g]["u", s][:]),
                 op0=ALU.add, op1=ALU.mult,
@@ -285,12 +327,12 @@ def tile_cfccell_pa_t_kernel(
 
         turn("ff2", None, 0); turn("ff2", None, 1)
         regroup("ff2", None, 0, on_scalar); regroup("ff2", None, 1, on_vector)
-        spread_biases()
         turn("ff1", 0, 0); turn("ff1", 0, 1)
         regroup("ff1", 0, 0, on_scalar); regroup("ff1", 0, 1, on_vector)
         quantise("ff2", None)
         quantise("ff1", 0)
         turn("in", None, 0); turn("in", None, 1)
+        spread_biases()
         regroup("in", None, 0, on_scalar); regroup("in", None, 1, on_vector)
         turn("x", 0, 0); turn("x", 0, 1)
         multiply("f", 0)
@@ -318,34 +360,46 @@ def tile_cfccell_pa_t_kernel(
             if g + 2 < N_GROUPS:
                 load_group(g + 2)
             if g > 0:
-                multiply("f", g, (0, 1))
-                turn("hx", g, 0); turn("hx", g, 1)
-                multiply("f", g, (2, 3))
+                multiply("f", g)
                 activate("f", g)
-                regroup("hx", g, 1, on_vector)
-                regroup("hx", g, 0, on_scalar)
-                gate(g - 1, PAIRS[0]); gate(g - 1, PAIRS[1])
+                turn("hx", g, 0); turn("hx", g, 1)
+                for s in row_blocks(g - 1): V_(g - 1, s)
+                regroup("hx", g, 0, on_scalar); regroup("hx", g, 1, on_scalar)
                 interleave(g)
                 quantise("hx", g)
                 quantise("h", g)
+                for s in row_blocks(g - 1): U_(g - 1, s)
                 multiply("i", g)
                 activate("i", g)
-            subtract(g, PAIRS[0])
+            subtract(g, PAIRS[0]); subtract(g, PAIRS[1])
             if not last:
                 turn("ff1", n, 0); turn("ff1", n, 1); turn("x", n, 0); turn("x", n, 1)
                 regroup("ff1", n, 0, on_scalar); regroup("ff1", n, 1, on_scalar)
-                regroup("x", n, 0, on_scalar); regroup("x", n, 1, on_scalar)
                 quantise("ff1", n)
+                regroup("x", n, 0, on_scalar); regroup("x", n, 1, on_scalar)
                 quantise("x", n)
             multiply("r", g)
             activate("r", g)
-            add(g, PAIRS[0], nc.vector)
-            subtract(g, PAIRS[1])
-            add(g, slice(2, 3), nc.gpsimd); add(g, slice(3, 4), nc.gpsimd)
+            add(g, PAIRS[0], nc.vector); add(g, PAIRS[1], nc.vector)
             if g > 0:
-                for s in FEATURE_BLOCKS: B_(g - 1, s); E_(g - 1, s)
+                if last:
+                    B_(g - 1, 0); B_(g - 1, 1); BX_(g - 1, 2); BX_(g - 1, 3)
+                    E_(g - 1, 0); EA_(g - 1, 2); EA_(g - 1, 3); E_(g - 1, 1)
+                else:
+                    for s in feature_blocks(g - 1): B_(g - 1, s); E_(g - 1, s)
+                for s in row_blocks(g - 1): H_(g - 1, s); W_(g - 1, s)
             multiply("t", g)
             activate("t", g)
+            if not last:
+                gate(g, PAIRS[0])
+            if g > 0:
+                for s in row_blocks(g - 1): Z_(g - 1, s)
+            if not last:
+                gate(g, PAIRS[1])
         g = N_GROUPS - 1
-        gate(g, PAIRS[0]); gate(g, PAIRS[1])
-        for s in FEATURE_BLOCKS: B_(g, s); E_(g, s)
+        gate_cols(g, 0)
+        BX_(g, 0); BX_(g, 1)
+        gate_cols(g, 1)
+        EA_(g, 0); EA_(g, 1)
+        B_(g, 2); BX_(g, 3)
+        E_(g, 2); EA_(g, 3)

@@ -24,6 +24,7 @@ HALF = GROUP // 2
 
 ROW_COUNT = (0, 0, 0, 0, 0, 0, 0, 0)
 PAIRS = (slice(0, 2), slice(2, 4))
+ALL = slice(0, 4)
 
 FLOPS = 5 * 2 * B * H * H
 
@@ -38,7 +39,7 @@ def tile_cfccell_pa_t_kernel(
         grouped_pool = stack.enter_context(tc.tile_pool(name="grouped", bufs=2))
         mx = stack.enter_context(tc.tile_pool(name="mx", bufs=2))
         work = stack.enter_context(tc.tile_pool(name="work", bufs=2))
-        store = stack.enter_context(tc.tile_pool(name="store", bufs=6))
+        store = stack.enter_context(tc.tile_pool(name="store", bufs=3))
         psum_t = stack.enter_context(tc.psum_pool(name="psum_t", bufs=4))
         psum_mx = stack.enter_context(tc.psum_pool(name="psum_mx", bufs=4))
         stack.enter_context(tc.manual_schedule())
@@ -208,7 +209,7 @@ def tile_cfccell_pa_t_kernel(
 
         def subtract(g, pair):
             FC = cols_of(g).stop
-            if pair == PAIRS[0]:
+            if pair.start == 0:
                 live[g]["delta"] = work.tile([P, CHUNKS, FC], F32, name="delta%d" % FC, bufs=2)
             delta = live[g]["delta"]
             grouped = operands["hx", g]["grouped"]
@@ -261,17 +262,24 @@ def tile_cfccell_pa_t_kernel(
         def B_(g, s):
             turn_back(g, s, [live[g]["delta"]], "back")
 
+        def result_block(g, s):
+            if "result" not in live[g]:
+                live[g]["result"] = store.tile([P, BLOCKS, H], F32, name="result")
+                live[g]["done"] = 0
+            return live[g]["result"][:, s, :]
+
+        def store_blocks(g, a, b):
+            nc.sync.dma_start(out=out_groups[g][:, a:b, :], in_=live[g]["result"][:, a:b, :])
+
         def E_(g, s):
-            result = store.tile([P, H], F32, name="result")
             nc.vector.scalar_tensor_tensor(
-                out=pairs_of(result[:]), in0=from_bank(g, "back", s), scalar=0.5, in1=pairs_of(hx_block(g, s)),
+                out=pairs_of(result_block(g, s)), in0=from_bank(g, "back", s), scalar=0.5, in1=pairs_of(hx_block(g, s)),
                 op0=ALU.mult, op1=ALU.add,
             )
-            nc.sync.dma_start(out=out_groups[g][:, s, :], in_=result[:])
 
-        def gate_cols(g, half):
+        def gate_block(g, s):
             delta = live[g]["delta"]
-            cols = slice(half * HALF, (half + 1) * HALF)
+            cols = slice(s * P, (s + 1) * P)
             nc.vector.scalar_tensor_tensor(
                 out=delta[:, :, cols], in0=live[g]["t"][:, :, cols], scalar=1.0, in1=delta[:, :, cols],
                 op0=ALU.add, op1=ALU.mult,
@@ -295,9 +303,7 @@ def tile_cfccell_pa_t_kernel(
             live[g]["back", s] = bank
 
         def EA_(g, s):
-            result = store.tile([P, H], F32, name="result")
-            nc.scalar.activation(out=pairs_of(result[:]), in_=from_bank(g, "back", s), func=ACT.Copy, scale=0.5)
-            nc.sync.dma_start(out=out_groups[g][:, s, :], in_=result[:])
+            nc.scalar.activation(out=pairs_of(result_block(g, s)), in_=from_bank(g, "back", s), func=ACT.Copy, scale=0.5)
 
         def V_(g, s):
             turn_back(g, s, [live[g]["i"], live[g]["r"]], "sum")
@@ -319,11 +325,9 @@ def tile_cfccell_pa_t_kernel(
             live[g]["w", s] = w
 
         def Z_(g, s):
-            result = store.tile([P, H], F32, name="result")
             nc.vector.scalar_tensor_tensor(
-                out=result[:], in0=live[g]["w", s][:], scalar=0.5, in1=hx_block(g, s), op0=ALU.mult, op1=ALU.add
+                out=result_block(g, s), in0=live[g]["w", s][:], scalar=0.5, in1=hx_block(g, s), op0=ALU.mult, op1=ALU.add
             )
-            nc.sync.dma_start(out=out_groups[g][:, s, :], in_=result[:])
 
         turn("ff2", None, 0); turn("ff2", None, 1)
         regroup("ff2", None, 0, on_scalar); regroup("ff2", None, 1, on_vector)
@@ -363,15 +367,13 @@ def tile_cfccell_pa_t_kernel(
                 multiply("f", g)
                 activate("f", g)
                 turn("hx", g, 0); turn("hx", g, 1)
-                for s in row_blocks(g - 1): V_(g - 1, s)
                 regroup("hx", g, 0, on_scalar); regroup("hx", g, 1, on_scalar)
                 interleave(g)
                 quantise("hx", g)
                 quantise("h", g)
-                for s in row_blocks(g - 1): U_(g - 1, s)
                 multiply("i", g)
                 activate("i", g)
-            subtract(g, PAIRS[0]); subtract(g, PAIRS[1])
+            subtract(g, ALL)
             if not last:
                 turn("ff1", n, 0); turn("ff1", n, 1); turn("x", n, 0); turn("x", n, 1)
                 regroup("ff1", n, 0, on_scalar); regroup("ff1", n, 1, on_scalar)
@@ -380,26 +382,30 @@ def tile_cfccell_pa_t_kernel(
                 quantise("x", n)
             multiply("r", g)
             activate("r", g)
-            add(g, PAIRS[0], nc.vector); add(g, PAIRS[1], nc.vector)
             if g > 0:
                 if last:
                     B_(g - 1, 0); B_(g - 1, 1); BX_(g - 1, 2); BX_(g - 1, 3)
-                    E_(g - 1, 0); EA_(g - 1, 2); EA_(g - 1, 3); E_(g - 1, 1)
+                    E_(g - 1, 0); add(g, ALL, nc.vector); EA_(g - 1, 2); EA_(g - 1, 3); E_(g - 1, 1)
+                    store_blocks(g - 1, 0, BLOCKS)
                 else:
-                    for s in feature_blocks(g - 1): B_(g - 1, s); E_(g - 1, s)
-                for s in row_blocks(g - 1): H_(g - 1, s); W_(g - 1, s)
+                    for s in (0, 1, 2): B_(g - 1, s); E_(g - 1, s)
+                    add(g, ALL, nc.vector)
+                    B_(g - 1, 3); E_(g - 1, 3)
+                    store_blocks(g - 1, 0, BLOCKS)
+            else:
+                add(g, ALL, nc.vector)
             multiply("t", g)
             activate("t", g)
             if not last:
-                gate(g, PAIRS[0])
-            if g > 0:
-                for s in row_blocks(g - 1): Z_(g - 1, s)
-            if not last:
-                gate(g, PAIRS[1])
+                gate(g, ALL)
         g = N_GROUPS - 1
-        gate_cols(g, 0)
-        BX_(g, 0); BX_(g, 1)
-        gate_cols(g, 1)
-        EA_(g, 0); EA_(g, 1)
-        B_(g, 2); BX_(g, 3)
-        E_(g, 2); EA_(g, 3)
+        for s in range(BLOCKS - 1):
+            gate_block(g, s)
+            BX_(g, s)
+        gate_block(g, 3)
+        B_(g, 3)
+        for s in range(BLOCKS - 1):
+            EA_(g, s)
+            store_blocks(g, s, s + 1)
+        E_(g, 3)
+        store_blocks(g, 3, 4)

@@ -90,10 +90,10 @@ def tile_cfccell_pa_t_kernel(
         nc.vector.memset(bias_rows[:], 0.0)
         load_weight("ff2", 2)
         load_rows("ff1", 0, 2)
-        for v, vec in enumerate(vectors):
-            nc.sync.dma_start(out=bias_rows[v : v + 1, :], in_=vec.rearrange("(o h) -> o h", o=1))
         load_weight("in")
         load_rows("x", 0)
+        for v, vec in enumerate(vectors):
+            nc.sync.dma_start(out=bias_rows[v : v + 1, :], in_=vec.rearrange("(o h) -> o h", o=1))
         load_weight("r")
         load_rows("hx", 0)
         load_weight("ta")
@@ -121,6 +121,14 @@ def tile_cfccell_pa_t_kernel(
             nc.vector.tensor_tensor(out=bias_gate_sum[:], in0=bias[:, 1, :], in1=bias[:, 2, :], op=ALU.add)
             nc.vector.tensor_scalar_mul(out=bias_gate[:], in0=bias_gate_sum[:], scalar1=0.5)
             chunk_bias["t"] = bias_gate[:]
+
+        warm_src = const.tile([P, GROUP], BF16, name="warm_src")
+        nc.vector.memset(warm_src[:], 0.0)
+
+        def warm(n):
+            for i in range(n):
+                bank = psum_mx.tile([P, GROUP], F32, tag="acc", name="acc")
+                nc.tensor.matmul(bank[:], lhsT=warm_src[:, 0:P], rhs=warm_src[:], start=True, stop=True)
 
         def turn(name, g, half):
             op = operands[name, g]
@@ -329,15 +337,19 @@ def tile_cfccell_pa_t_kernel(
                 out=result_block(g, s), in0=live[g]["w", s][:], scalar=0.5, in1=hx_block(g, s), op0=ALU.mult, op1=ALU.add
             )
 
+        warm(5)
         turn("ff2", None, 0); turn("ff2", None, 1)
+        warm(2)
         regroup("ff2", None, 0, on_scalar); regroup("ff2", None, 1, on_vector)
         turn("ff1", 0, 0); turn("ff1", 0, 1)
         regroup("ff1", 0, 0, on_scalar); regroup("ff1", 0, 1, on_vector)
         quantise("ff2", None)
         quantise("ff1", 0)
+        warm(2)
         turn("in", None, 0); turn("in", None, 1)
         spread_biases()
         regroup("in", None, 0, on_scalar); regroup("in", None, 1, on_vector)
+        warm(0)
         turn("x", 0, 0); turn("x", 0, 1)
         multiply("f", 0)
         regroup("x", 0, 0, on_scalar)
@@ -368,8 +380,8 @@ def tile_cfccell_pa_t_kernel(
                 activate("f", g)
                 turn("hx", g, 0); turn("hx", g, 1)
                 regroup("hx", g, 0, on_scalar); regroup("hx", g, 1, on_scalar)
-                interleave(g)
                 quantise("hx", g)
+                interleave(g)
                 quantise("h", g)
                 multiply("i", g)
                 activate("i", g)

@@ -46,8 +46,8 @@ def tile_cfccell_pa_t_kernel(
 
         ident = const.tile([P, P], F32, name="ident")
         make_identity(nc, ident[:])
-        twice = const.tile([P, P], BF16, name="twice")
-        nc.vector.tensor_scalar_mul(out=twice[:], in0=ident[:], scalar1=2.0)
+        warm_src = const.tile([P, GROUP], BF16, name="warm_src")
+        nc.vector.memset(warm_src[:].bitcast(U32), 0)
         warm_in = const.tile([P, 1], F32, name="warm_in")
         warm_out = const.tile([P, 1], F32, name="warm_out")
         nc.vector.memset(warm_in[:], 0.0)
@@ -87,7 +87,7 @@ def tile_cfccell_pa_t_kernel(
 
         vectors = (b_ff2, b_ta, b_tb, b_in, input_b, r_b)
         bias_rows = const.tile([P, H], BF16, name="bias_rows")
-        nc.vector.memset(bias_rows[:], 0.0)
+        nc.vector.memset(bias_rows[:].bitcast(U32), 0)
         load_weight("ff2", 2)
         load_rows("ff1", 0, 2)
         load_weight("in")
@@ -122,18 +122,23 @@ def tile_cfccell_pa_t_kernel(
             nc.vector.tensor_scalar_mul(out=bias_gate[:], in0=bias_gate_sum[:], scalar1=0.5)
             chunk_bias["t"] = bias_gate[:]
 
-        warm_src = const.tile([P, GROUP], BF16, name="warm_src")
-        nc.vector.memset(warm_src[:], 0.0)
+        twice = const.tile([P, P], BF16, name="twice")
+        nc.vector.tensor_scalar_mul(out=twice[:], in0=ident[:], scalar1=2.0)
 
         def warm(n):
             for i in range(n):
                 bank = psum_mx.tile([P, GROUP], F32, tag="acc", name="acc")
                 nc.tensor.matmul(bank[:], lhsT=warm_src[:, 0:P], rhs=warm_src[:], start=True, stop=True)
 
-        def turn(name, g, half):
+        def keep_warm(bank):
+            nc.tensor.matmul(bank, lhsT=warm_src[:, 0:P], rhs=warm_src[:], start=True, stop=True)
+
+        def turn(name, g, half, w=0):
             op = operands[name, g]
             words = op["rows"][:].bitcast(F32)
             planes = psum_t.tile([P, 2, HALF], F32, tag="transposed", name="planes")
+            for i in range(w):
+                keep_warm(planes[:].rearrange("p u c -> p (u c)"))
             for s in range(2):
                 slot = 2 * half + s
                 for u in range(2):
@@ -249,8 +254,10 @@ def tile_cfccell_pa_t_kernel(
         def hx_block(g, s):
             return operands["hx", g]["rows"][:, s * H : (s + 1) * H]
 
-        def turn_back(g, s, terms, key):
+        def turn_back(g, s, terms, key, w=0):
             bank = psum_t.tile([P, H], F32, tag="transposed", name=key)
+            for i in range(w):
+                keep_warm(bank[:])
             for c in range(CHUNKS):
                 u, e = divmod(c, 2)
                 for i, term in enumerate(terms):
@@ -267,8 +274,8 @@ def tile_cfccell_pa_t_kernel(
         def from_bank(g, key, s):
             return live[g][key, s][:].rearrange("b (e q) -> b q e", e=2)
 
-        def B_(g, s):
-            turn_back(g, s, [live[g]["delta"]], "back")
+        def B_(g, s, w=0):
+            turn_back(g, s, [live[g]["delta"]], "back", w)
 
         def result_block(g, s):
             if "result" not in live[g]:
@@ -373,18 +380,18 @@ def tile_cfccell_pa_t_kernel(
         for g in range(N_GROUPS):
             n = g + 1
             last = n == N_GROUPS
-            if g + 2 < N_GROUPS:
-                load_group(g + 2)
             if g > 0:
                 multiply("f", g)
                 activate("f", g)
                 turn("hx", g, 0); turn("hx", g, 1)
                 regroup("hx", g, 0, on_scalar); regroup("hx", g, 1, on_scalar)
-                quantise("hx", g)
                 interleave(g)
+                quantise("hx", g)
                 quantise("h", g)
                 multiply("i", g)
                 activate("i", g)
+            if g + 2 < N_GROUPS:
+                load_group(g + 2)
             subtract(g, ALL)
             if not last:
                 turn("ff1", n, 0); turn("ff1", n, 1); turn("x", n, 0); turn("x", n, 1)
@@ -400,7 +407,8 @@ def tile_cfccell_pa_t_kernel(
                     E_(g - 1, 0); add(g, ALL, nc.vector); EA_(g - 1, 2); EA_(g - 1, 3); E_(g - 1, 1)
                     store_blocks(g - 1, 0, BLOCKS)
                 else:
-                    for s in (0, 1, 2): B_(g - 1, s); E_(g - 1, s)
+                    B_(g - 1, 0); E_(g - 1, 0); B_(g - 1, 1); E_(g - 1, 1)
+                    BX_(g - 1, 2); EA_(g - 1, 2)
                     add(g, ALL, nc.vector)
                     B_(g - 1, 3); E_(g - 1, 3)
                     store_blocks(g - 1, 0, BLOCKS)

@@ -222,12 +222,12 @@ def tile_cfccell_pa_t_kernel(
 
         def subtract(g, pair):
             FC = cols_of(g).stop
-            if pair.start == 0:
-                live[g]["delta"] = work.tile([P, CHUNKS, FC], F32, name="delta%d" % FC, bufs=2)
+            if "delta" not in live[g]:
+                live[g]["delta"] = work.tile([P, CHUNKS, GROUP], F32, tag="delta", name="delta", bufs=2)
             delta = live[g]["delta"]
             grouped = operands["hx", g]["grouped"]
             nc.vector.tensor_tensor(
-                out=delta[:, pair, :],
+                out=delta[:, pair, 0:FC],
                 in0=live[g]["i"][:, pair, 0:FC],
                 in1=grouped[:, 0 : FC * PACK].rearrange("p (b j) -> p j b", j=PACK)[:, pair, :],
                 op=ALU.subtract,
@@ -236,13 +236,13 @@ def tile_cfccell_pa_t_kernel(
         def add(g, chunks, engine):
             FC = cols_of(g).stop
             delta = live[g]["delta"]
-            engine.tensor_tensor(out=delta[:, chunks, :], in0=delta[:, chunks, :], in1=live[g]["r"][:, chunks, 0:FC], op=ALU.add)
+            engine.tensor_tensor(out=delta[:, chunks, 0:FC], in0=delta[:, chunks, 0:FC], in1=live[g]["r"][:, chunks, 0:FC], op=ALU.add)
 
         def gate(g, pair):
             FC = cols_of(g).stop
             delta = live[g]["delta"]
             nc.vector.scalar_tensor_tensor(
-                out=delta[:, pair, :], in0=live[g]["t"][:, pair, 0:FC], scalar=1.0, in1=delta[:, pair, :],
+                out=delta[:, pair, 0:FC], in0=live[g]["t"][:, pair, 0:FC], scalar=1.0, in1=delta[:, pair, 0:FC],
                 op0=ALU.add, op1=ALU.mult,
             )
 
@@ -317,6 +317,33 @@ def tile_cfccell_pa_t_kernel(
                 )
             live[g]["back", s] = bank
 
+        def open_bank(g, s):
+            bank = psum_t.tile([P, H], F32, tag="transposed", name="back")
+            nc.tensor.matmul(
+                bank[:], lhsT=twice[:], rhs=hx_block(g, s).rearrange("b (q e) -> b e q", e=2), start=True, stop=False
+            )
+            live[g]["back", s] = bank
+
+        def add_back(g, s, term, c, stop):
+            u, e = divmod(c, 2)
+            nc.tensor.matmul(
+                live[g]["back", s][:, e * WORDS + u * P : e * WORDS + (u + 1) * P],
+                lhsT=term[:, c, s * P : (s + 1) * P],
+                rhs=ident[:],
+                is_transpose=True,
+                start=False,
+                stop=stop,
+            )
+
+        def gate_rec(g, c):
+            rec = live[g]["r"]
+            nc.vector.scalar_tensor_tensor(
+                out=rec[:, c, :], in0=live[g]["t"][:, c, :], scalar=1.0, in1=rec[:, c, :], op0=ALU.add, op1=ALU.mult
+            )
+
+        def ES_(g, s):
+            nc.vector.tensor_scalar_mul(out=pairs_of(result_block(g, s)), in0=from_bank(g, "back", s), scalar1=0.5)
+
         def EA_(g, s):
             nc.scalar.activation(out=pairs_of(result_block(g, s)), in_=from_bank(g, "back", s), func=ACT.Copy, scale=0.5)
 
@@ -384,7 +411,7 @@ def tile_cfccell_pa_t_kernel(
                 multiply("f", g)
                 activate("f", g)
                 turn("hx", g, 0); turn("hx", g, 1)
-                regroup("hx", g, 0, on_scalar); regroup("hx", g, 1, on_scalar)
+                regroup("hx", g, 0, on_scalar); regroup("hx", g, 1, on_vector if g % 2 and not last else on_scalar)
                 interleave(g)
                 quantise("hx", g)
                 quantise("h", g)
@@ -392,13 +419,14 @@ def tile_cfccell_pa_t_kernel(
                 activate("i", g)
             if g + 2 < N_GROUPS:
                 load_group(g + 2)
-            subtract(g, ALL)
+            subtract(g, slice(1, 4) if 0 < g < N_GROUPS - 1 else ALL)
             if not last:
                 turn("ff1", n, 0); turn("ff1", n, 1); turn("x", n, 0); turn("x", n, 1)
                 regroup("ff1", n, 0, on_scalar); regroup("ff1", n, 1, on_scalar)
                 quantise("ff1", n)
                 regroup("x", n, 0, on_scalar); regroup("x", n, 1, on_scalar)
-                quantise("x", n)
+                if g == 0:
+                    quantise("x", n)
             multiply("r", g)
             activate("r", g)
             if g > 0:
@@ -407,11 +435,14 @@ def tile_cfccell_pa_t_kernel(
                     E_(g - 1, 0); add(g, ALL, nc.vector); EA_(g - 1, 2); EA_(g - 1, 3); E_(g - 1, 1)
                     store_blocks(g - 1, 0, BLOCKS)
                 else:
+                    subtract(g, slice(0, 1))
+                    add(g, slice(0, 1), nc.gpsimd)
                     B_(g - 1, 0); E_(g - 1, 0); B_(g - 1, 1); E_(g - 1, 1)
-                    BX_(g - 1, 2); EA_(g - 1, 2)
-                    add(g, ALL, nc.vector)
                     B_(g - 1, 3); E_(g - 1, 3)
+                    BX_(g - 1, 2); EA_(g - 1, 2)
                     store_blocks(g - 1, 0, BLOCKS)
+                    add(g, slice(1, 4), nc.vector)
+                    quantise("x", n)
             else:
                 add(g, ALL, nc.vector)
             multiply("t", g)

@@ -113,12 +113,20 @@ def tile_cfccell_pa_t_kernel(
             )
             chunk_bias["f"] = bias[:, 0, :]
             chunk_bias["r"] = bias[:, 5, :]
+            chunk_bias["all"] = bias
+
+        def finish_biases():
+            bias = chunk_bias["all"]
             bias_in = const.tile([P, CHUNKS], F32, name="bias_in")
             nc.vector.tensor_tensor(out=bias_in[:], in0=bias[:, 3, :], in1=bias[:, 4, :], op=ALU.add)
             chunk_bias["i"] = bias_in[:]
             bias_gate_sum = const.tile([P, CHUNKS], F32, name="bias_gate_sum")
-            bias_gate = const.tile([P, CHUNKS], F32, name="bias_gate")
             nc.vector.tensor_tensor(out=bias_gate_sum[:], in0=bias[:, 1, :], in1=bias[:, 2, :], op=ALU.add)
+            chunk_bias["gate_sum"] = bias_gate_sum
+
+        def halve_gate_bias():
+            bias_gate_sum = chunk_bias["gate_sum"]
+            bias_gate = const.tile([P, CHUNKS], F32, name="bias_gate")
             nc.vector.tensor_scalar_mul(out=bias_gate[:], in0=bias_gate_sum[:], scalar1=0.5)
             chunk_bias["t"] = bias_gate[:]
 
@@ -154,7 +162,7 @@ def tile_cfccell_pa_t_kernel(
             if "grouped" not in op:
                 tag = "hx_grouped" if name == "hx" else "grouped"
                 op["grouped"] = grouped_pool.tile(
-                    [P, GROUP * PACK], BF16, align_bytes=64, tag=tag, name=tag, bufs=2 if name == "hx" else 3
+                    [P, GROUP * PACK], BF16, align_bytes=64, tag=tag, name=tag, bufs=2 if name == "hx" else 4
                 )
             words = op["grouped"][:].bitcast(F32).rearrange("p (c u) -> p c u", u=2)
             copy(
@@ -300,8 +308,10 @@ def tile_cfccell_pa_t_kernel(
                 op0=ALU.add, op1=ALU.mult,
             )
 
-        def BX_(g, s):
+        def BX_(g, s, w=0):
             bank = psum_t.tile([P, H], F32, tag="transposed", name="back")
+            for i in range(w):
+                keep_warm(bank[:])
             nc.tensor.matmul(
                 bank[:], lhsT=twice[:], rhs=hx_block(g, s).rearrange("b (q e) -> b e q", e=2), start=True, stop=False
             )
@@ -371,7 +381,7 @@ def tile_cfccell_pa_t_kernel(
                 out=result_block(g, s), in0=live[g]["w", s][:], scalar=0.5, in1=hx_block(g, s), op0=ALU.mult, op1=ALU.add
             )
 
-        warm(5)
+        warm(3)
         turn("ff2", None, 0); turn("ff2", None, 1)
         warm(2)
         regroup("ff2", None, 0, on_scalar); regroup("ff2", None, 1, on_vector)
@@ -381,22 +391,27 @@ def tile_cfccell_pa_t_kernel(
         quantise("ff1", 0)
         warm(2)
         turn("in", None, 0); turn("in", None, 1)
-        spread_biases()
-        regroup("in", None, 0, on_scalar); regroup("in", None, 1, on_vector)
-        warm(0)
+        regroup("in", None, 0, on_scalar)
+        regroup("in", None, 1, on_vector)
         turn("x", 0, 0); turn("x", 0, 1)
+        spread_biases()
         multiply("f", 0)
         regroup("x", 0, 0, on_scalar)
-        quantise("in", None)
         regroup("x", 0, 1, on_vector)
-        activate("f", 0)
+        quantise("in", None)
+        finish_biases()
         quantise("x", 0)
-        turn("r", None, 0); turn("r", None, 1); turn("hx", 0, 0); turn("hx", 0, 1)
+        halve_gate_bias()
+        activate("f", 0)
+        turn("r", None, 0); turn("r", None, 1)
         multiply("i", 0)
+        turn("hx", 0, 0); turn("hx", 0, 1)
         regroup("r", None, 0, on_vector); regroup("r", None, 1, on_vector)
-        regroup("hx", 0, 0, on_scalar); regroup("hx", 0, 1, on_vector)
-        activate("i", 0)
+        activate("i", 0, (0, 1, 2))
+        regroup("hx", 0, 0, on_scalar)
+        activate("i", 0, (3,))
         interleave(0)
+        regroup("hx", 0, 1, on_vector)
         quantise("r", None)
         quantise("hx", 0)
         turn("ta", None, 0); turn("ta", None, 1); turn("tb", None, 0); turn("tb", None, 1)
@@ -411,7 +426,7 @@ def tile_cfccell_pa_t_kernel(
                 multiply("f", g)
                 activate("f", g)
                 turn("hx", g, 0); turn("hx", g, 1)
-                regroup("hx", g, 0, on_scalar); regroup("hx", g, 1, on_vector if g % 2 and not last else on_scalar)
+                regroup("hx", g, 0, on_scalar); regroup("hx", g, 1, on_scalar if last else on_vector)
                 interleave(g)
                 quantise("hx", g)
                 quantise("h", g)
@@ -419,6 +434,9 @@ def tile_cfccell_pa_t_kernel(
                 activate("i", g)
             if g + 2 < N_GROUPS:
                 load_group(g + 2)
+            if last:
+                B_(g - 1, 0); B_(g - 1, 1)
+                E_(g - 1, 0)
             subtract(g, slice(1, 4) if 0 < g < N_GROUPS - 1 else ALL)
             if not last:
                 turn("ff1", n, 0); turn("ff1", n, 1); turn("x", n, 0); turn("x", n, 1)
@@ -430,11 +448,7 @@ def tile_cfccell_pa_t_kernel(
             multiply("r", g)
             activate("r", g)
             if g > 0:
-                if last:
-                    B_(g - 1, 0); B_(g - 1, 1); BX_(g - 1, 2); BX_(g - 1, 3)
-                    E_(g - 1, 0); add(g, ALL, nc.vector); EA_(g - 1, 2); EA_(g - 1, 3); E_(g - 1, 1)
-                    store_blocks(g - 1, 0, BLOCKS)
-                else:
+                if not last:
                     subtract(g, slice(0, 1))
                     add(g, slice(0, 1), nc.gpsimd)
                     B_(g - 1, 0); E_(g - 1, 0); B_(g - 1, 1); E_(g - 1, 1)
@@ -445,14 +459,23 @@ def tile_cfccell_pa_t_kernel(
                     quantise("x", n)
             else:
                 add(g, ALL, nc.vector)
+            if last:
+                E_(g - 1, 1)
+                store_blocks(g - 1, 0, 2)
+                add(g, ALL, nc.vector)
             multiply("t", g)
+            if last:
+                BX_(g - 1, 2); BX_(g - 1, 3)
             activate("t", g)
             if not last:
                 gate(g, ALL)
         g = N_GROUPS - 1
+        EA_(g - 1, 2)
+        EA_(g - 1, 3)
+        store_blocks(g - 1, 2, BLOCKS)
         for s in range(BLOCKS - 1):
             gate_block(g, s)
-            BX_(g, s)
+            BX_(g, s, 4 if s == 0 else 0)
         gate_block(g, 3)
         B_(g, 3)
         for s in range(BLOCKS - 1):

from contextlib import ExitStack

import concourse.mybir as mybir
from concourse.masks import make_identity

F32 = mybir.dt.float32
BF16 = mybir.dt.bfloat16
U32 = mybir.dt.uint32
U8 = mybir.dt.uint8
FP8X4 = mybir.dt.float8_e4m3fn_x4
ACT = mybir.ActivationFunctionType
ALU = mybir.AluOpType

P = 128
PACK = 4
B = 4096
H = 512
GROUP = 512
BLOCKS = GROUP // P
CHUNKS = H // P
N_GROUPS = B // GROUP
WORDS = H // 2
HALF = GROUP // 2

ROW_COUNT = (0, 0, 0, 0, 0, 0, 0, 0)
PAIRS = (slice(0, 2), slice(2, 4))
ALL = slice(0, 4)

FLOPS = 5 * 2 * B * H * H


def tile_cfccell_pa_t_kernel(
    tc, ff1, x, hx, W_ff2, b_ff2, W_ta, b_ta, W_tb, b_tb, W_in, b_in, input_b, W_r, r_b, out
):
    nc = tc.nc
    with ExitStack() as stack:
        const = stack.enter_context(tc.tile_pool(name="const", bufs=1))
        rows_pool = stack.enter_context(tc.tile_pool(name="rows", bufs=4))
        grouped_pool = stack.enter_context(tc.tile_pool(name="grouped", bufs=2))
        mx = stack.enter_context(tc.tile_pool(name="mx", bufs=2))
        work = stack.enter_context(tc.tile_pool(name="work", bufs=2))
        store = stack.enter_context(tc.tile_pool(name="store", bufs=3))
        psum_t = stack.enter_context(tc.psum_pool(name="psum_t", bufs=4))
        psum_mx = stack.enter_context(tc.psum_pool(name="psum_mx", bufs=4))
        stack.enter_context(tc.manual_schedule())

        ident = const.tile([P, P], F32, name="ident")
        make_identity(nc, ident[:])
        warm_src = const.tile([P, GROUP], BF16, name="warm_src")
        nc.vector.memset(warm_src[:].bitcast(U32), 0)
        warm_in = const.tile([P, 1], F32, name="warm_in")
        warm_out = const.tile([P, 1], F32, name="warm_out")
        nc.vector.memset(warm_in[:], 0.0)
        nc.scalar.activation(out=warm_out[:], in_=warm_in[:], func=ACT.Gelu)

        on_scalar = nc.scalar.copy
        on_vector = nc.vector.tensor_copy
        live = {g: {} for g in range(N_GROUPS)}
        sources = {"ff1": ff1, "x": x, "hx": hx}
        weights = {"ff2": W_ff2, "in": W_in, "r": W_r, "ta": W_ta, "tb": W_tb}
        operands = {}

        def load_rows(name, g, pieces=1):
            rows = rows_pool.tile([P, BLOCKS * H], BF16, tag=name, name=name)
            run = BLOCKS * H // pieces
            for i in range(pieces):
                nc.sync.dma_start(
                    out=rows[:, i * run : (i + 1) * run],
                    in_=sources[name].rearrange("(g p s) k -> g p (s k)", p=P, s=BLOCKS)[g][:, i * run : (i + 1) * run],
                )
            operands[name, g] = {"rows": rows}

        def load_group(g):
            for name in ("ff1", "x", "hx"):
                load_rows(name, g)

        def load_weight(name, pieces=1):
            rows = const.tile([P, CHUNKS * H], BF16, name="rows_" + name)
            step = 2 // pieces
            for i in range(pieces):
                u = slice(i * step, (i + 1) * step)
                nc.sync.dma_start(
                    out=rows[:].rearrange("r (u ek) -> r u ek", u=2)[:, u, :],
                    in_=weights[name].rearrange("(u r e) k -> r u (e k)", u=2, e=2)[:, u, :],
                )
            operands[name, None] = {"rows": rows}

        vectors = (b_ff2, b_ta, b_tb, b_in, input_b, r_b)
        bias_rows = const.tile([P, H], BF16, name="bias_rows")
        nc.vector.memset(bias_rows[:].bitcast(U32), 0)
        load_weight("ff2", 2)
        load_rows("ff1", 0, 2)
        load_weight("in")
        load_rows("x", 0)
        for v, vec in enumerate(vectors):
            nc.sync.dma_start(out=bias_rows[v : v + 1, :], in_=vec.rearrange("(o h) -> o h", o=1))
        load_weight("r")
        load_rows("hx", 0)
        load_weight("ta")
        load_weight("tb")
        load_group(1)

        chunk_bias = {}

        def spread_biases():
            bias_planes = psum_t.tile([P, 2, P], F32, tag="transposed", name="bias_planes")
            for u in range(2):
                nc.tensor.transpose(bias_planes[:, u, :], bias_rows[:].bitcast(F32)[:, u * P : (u + 1) * P], ident[:])
            bias = const.tile([P, len(vectors), CHUNKS], F32, name="bias")
            nc.vector.tensor_copy(
                out=bias[:].rearrange("p v (u e) -> p v u e", e=2),
                in_=bias_planes[:].bitcast(BF16)[:, :, 0 : 2 * len(vectors)].rearrange("p u (v e) -> p v u e", e=2),
            )
            chunk_bias["f"] = bias[:, 0, :]
            chunk_bias["r"] = bias[:, 5, :]
            chunk_bias["all"] = bias

        def finish_biases():
            bias = chunk_bias["all"]
            bias_in = const.tile([P, CHUNKS], F32, name="bias_in")
            nc.vector.tensor_tensor(out=bias_in[:], in0=bias[:, 3, :], in1=bias[:, 4, :], op=ALU.add)
            chunk_bias["i"] = bias_in[:]
            bias_gate_sum = const.tile([P, CHUNKS], F32, name="bias_gate_sum")
            nc.vector.tensor_tensor(out=bias_gate_sum[:], in0=bias[:, 1, :], in1=bias[:, 2, :], op=ALU.add)
            chunk_bias["gate_sum"] = bias_gate_sum

        def halve_gate_bias():
            bias_gate_sum = chunk_bias["gate_sum"]
            bias_gate = const.tile([P, CHUNKS], F32, name="bias_gate")
            nc.vector.tensor_scalar_mul(out=bias_gate[:], in0=bias_gate_sum[:], scalar1=0.5)
            chunk_bias["t"] = bias_gate[:]

        twice = const.tile([P, P], BF16, name="twice")
        nc.vector.tensor_scalar_mul(out=twice[:], in0=ident[:], scalar1=2.0)

        def warm(n):
            for i in range(n):
                bank = psum_mx.tile([P, GROUP], F32, tag="acc", name="acc")
                nc.tensor.matmul(bank[:], lhsT=warm_src[:, 0:P], rhs=warm_src[:], start=True, stop=True)

        def keep_warm(bank):
            nc.tensor.matmul(bank, lhsT=warm_src[:, 0:P], rhs=warm_src[:], start=True, stop=True)

        def turn(name, g, half, w=0):
            op = operands[name, g]
            words = op["rows"][:].bitcast(F32)
            planes = psum_t.tile([P, 2, HALF], F32, tag="transposed", name="planes")
            for i in range(w):
                keep_warm(planes[:].rearrange("p u c -> p (u c)"))
            for s in range(2):
                slot = 2 * half + s
                for u in range(2):
                    nc.tensor.transpose(
                        planes[:, u, s * P : (s + 1) * P],
                        words[:, slot * WORDS + u * P : slot * WORDS + (u + 1) * P],
                        ident[:],
                    )
            op["planes", half] = planes

        def regroup(name, g, half, copy):
            op = operands[name, g]
            if "grouped" not in op:
                tag = "hx_grouped" if name == "hx" else "grouped"
                op["grouped"] = grouped_pool.tile(
                    [P, GROUP * PACK], BF16, align_bytes=64, tag=tag, name=tag, bufs=2 if name == "hx" else 4
                )
            words = op["grouped"][:].bitcast(F32).rearrange("p (c u) -> p c u", u=2)
            copy(
                out=words[:, half * HALF : (half + 1) * HALF, :],
                in_=op["planes", half][:].rearrange("p u c -> p c u"),
            )

        def quantise(name, g):
            op = operands[name, g]
            pool = const if g is None else mx
            op["codes"] = pool.tile([P, GROUP], U32, align_bytes=64, tag="codes_" + name, name="codes_" + name)
            op["scales"] = pool.tile([P, GROUP], U8, align_bytes=64, tag="scales_" + name, name="scales_" + name)
            nc.vector.quantize_mx(out=op["codes"][:].bitcast(FP8X4), scales=op["scales"][:], in_=op["grouped"][:])

        stages = {"f": ("ff1", ("ff2",)), "i": ("x", ("in",)), "r": ("hx", ("r",)), "t": ("h", ("ta", "tb"))}

        def multiply(stage, g, chunks=range(CHUNKS)):
            moving, names = stages[stage]
            op = operands[moving, g]
            for c in chunks:
                acc = psum_mx.tile([P, GROUP], F32, tag="acc", name="acc")
                for i, name in enumerate(names):
                    w = operands[name, None]
                    nc.tensor.matmul_mx(
                        out=acc[:],
                        lhsT=w["codes"][:, c * P : (c + 1) * P].bitcast(FP8X4),
                        lhsT_scale=w["scales"][:, c * P : (c + 1) * P],
                        rhs=op["codes"][:].bitcast(FP8X4),
                        rhs_scale=op["scales"][:],
                        start=(i == 0),
                        stop=(i == len(names) - 1),
                    )
                live[g][stage, c] = acc

        def activate(stage, g, chunks=range(CHUNKS)):
            for c in chunks:
                if c == 0:
                    live[g][stage] = work.tile(
                        [P, CHUNKS, GROUP], BF16 if stage == "f" else F32, tag="act_" + stage, name="act_" + stage
                    )
                nc.scalar.activation(
                    out=live[g][stage][:, c, :],
                    in_=live[g][stage, c][:],
                    func=ACT.Tanh if stage == "t" else ACT.Gelu,
                    bias=chunk_bias[stage][:, c : c + 1],
                    scale=0.5 if stage == "t" else 1.0,
                )

        def interleave(g):
            grouped = grouped_pool.tile([P, GROUP * PACK], BF16, align_bytes=64, tag="ff2_grouped", name="ff2_grouped", bufs=2)
            nc.vector.tensor_copy(
                out=grouped[:].rearrange("p (b i j) -> p b j i", i=4, j=PACK),
                in_=live[g]["f"][:].rearrange("p j (b i) -> p b j i", i=4),
            )
            operands["h", g] = {"grouped": grouped}

        def row_blocks(g):
            return range(BLOCKS - ROW_COUNT[g], BLOCKS)

        def feature_blocks(g):
            return range(BLOCKS - ROW_COUNT[g])

        def cols_of(g):
            return slice(0, (BLOCKS - ROW_COUNT[g]) * P)

        def subtract(g, pair):
            FC = cols_of(g).stop
            if "delta" not in live[g]:
                live[g]["delta"] = work.tile([P, CHUNKS, GROUP], F32, tag="delta", name="delta", bufs=2)
            delta = live[g]["delta"]
            grouped = operands["hx", g]["grouped"]
            nc.vector.tensor_tensor(
                out=delta[:, pair, 0:FC],
                in0=live[g]["i"][:, pair, 0:FC],
                in1=grouped[:, 0 : FC * PACK].rearrange("p (b j) -> p j b", j=PACK)[:, pair, :],
                op=ALU.subtract,
            )

        def add(g, chunks, engine):
            FC = cols_of(g).stop
            delta = live[g]["delta"]
            engine.tensor_tensor(out=delta[:, chunks, 0:FC], in0=delta[:, chunks, 0:FC], in1=live[g]["r"][:, chunks, 0:FC], op=ALU.add)

        def gate(g, pair):
            FC = cols_of(g).stop
            delta = live[g]["delta"]
            nc.vector.scalar_tensor_tensor(
                out=delta[:, pair, 0:FC], in0=live[g]["t"][:, pair, 0:FC], scalar=1.0, in1=delta[:, pair, 0:FC],
                op0=ALU.add, op1=ALU.mult,
            )

        out_groups = out.rearrange("(g p s) f -> g p s f", p=P, s=BLOCKS)

        def pairs_of(ap):
            return ap.rearrange("b (q e) -> b q e", e=2)

        def hx_block(g, s):
            return operands["hx", g]["rows"][:, s * H : (s + 1) * H]

        def turn_back(g, s, terms, key, w=0):
            bank = psum_t.tile([P, H], F32, tag="transposed", name=key)
            for i in range(w):
                keep_warm(bank[:])
            for c in range(CHUNKS):
                u, e = divmod(c, 2)
                for i, term in enumerate(terms):
                    nc.tensor.matmul(
                        bank[:, e * WORDS + u * P : e * WORDS + (u + 1) * P],
                        lhsT=term[:, c, s * P : (s + 1) * P],
                        rhs=ident[:],
                        is_transpose=True,
                        start=(i == 0),
                        stop=(i == len(terms) - 1),
                    )
            live[g][key, s] = bank

        def from_bank(g, key, s):
            return live[g][key, s][:].rearrange("b (e q) -> b q e", e=2)

        def B_(g, s, w=0):
            turn_back(g, s, [live[g]["delta"]], "back", w)

        def result_block(g, s):
            if "result" not in live[g]:
                live[g]["result"] = store.tile([P, BLOCKS, H], F32, name="result")
                live[g]["done"] = 0
            return live[g]["result"][:, s, :]

        def store_blocks(g, a, b):
            nc.sync.dma_start(out=out_groups[g][:, a:b, :], in_=live[g]["result"][:, a:b, :])

        def E_(g, s):
            nc.vector.scalar_tensor_tensor(
                out=pairs_of(result_block(g, s)), in0=from_bank(g, "back", s), scalar=0.5, in1=pairs_of(hx_block(g, s)),
                op0=ALU.mult, op1=ALU.add,
            )

        def gate_block(g, s):
            delta = live[g]["delta"]
            cols = slice(s * P, (s + 1) * P)
            nc.vector.scalar_tensor_tensor(
                out=delta[:, :, cols], in0=live[g]["t"][:, :, cols], scalar=1.0, in1=delta[:, :, cols],
                op0=ALU.add, op1=ALU.mult,
            )

        def BX_(g, s, w=0):
            bank = psum_t.tile([P, H], F32, tag="transposed", name="back")
            for i in range(w):
                keep_warm(bank[:])
            nc.tensor.matmul(
                bank[:], lhsT=twice[:], rhs=hx_block(g, s).rearrange("b (q e) -> b e q", e=2), start=True, stop=False
            )
            for c in range(CHUNKS):
                u, e = divmod(c, 2)
                nc.tensor.matmul(
                    bank[:, e * WORDS + u * P : e * WORDS + (u + 1) * P],
                    lhsT=live[g]["delta"][:, c, s * P : (s + 1) * P],
                    rhs=ident[:],
                    is_transpose=True,
                    start=False,
                    stop=(c == CHUNKS - 1),
                )
            live[g]["back", s] = bank

        def open_bank(g, s):
            bank = psum_t.tile([P, H], F32, tag="transposed", name="back")
            nc.tensor.matmul(
                bank[:], lhsT=twice[:], rhs=hx_block(g, s).rearrange("b (q e) -> b e q", e=2), start=True, stop=False
            )
            live[g]["back", s] = bank

        def add_back(g, s, term, c, stop):
            u, e = divmod(c, 2)
            nc.tensor.matmul(
                live[g]["back", s][:, e * WORDS + u * P : e * WORDS + (u + 1) * P],
                lhsT=term[:, c, s * P : (s + 1) * P],
                rhs=ident[:],
                is_transpose=True,
                start=False,
                stop=stop,
            )

        def gate_rec(g, c):
            rec = live[g]["r"]
            nc.vector.scalar_tensor_tensor(
                out=rec[:, c, :], in0=live[g]["t"][:, c, :], scalar=1.0, in1=rec[:, c, :], op0=ALU.add, op1=ALU.mult
            )

        def ES_(g, s):
            nc.vector.tensor_scalar_mul(out=pairs_of(result_block(g, s)), in0=from_bank(g, "back", s), scalar1=0.5)

        def EA_(g, s):
            nc.scalar.activation(out=pairs_of(result_block(g, s)), in_=from_bank(g, "back", s), func=ACT.Copy, scale=0.5)

        def V_(g, s):
            turn_back(g, s, [live[g]["i"], live[g]["r"]], "sum")

        def U_(g, s):
            u = store.tile([P, H], F32, name="u", bufs=3)
            nc.vector.tensor_tensor(out=pairs_of(u[:]), in0=from_bank(g, "sum", s), in1=pairs_of(hx_block(g, s)), op=ALU.subtract)
            live[g]["u", s] = u

        def H_(g, s):
            turn_back(g, s, [live[g]["t"]], "gate")

        def W_(g, s):
            w = store.tile([P, H], F32, name="w", bufs=2)
            nc.vector.scalar_tensor_tensor(
                out=pairs_of(w[:]), in0=from_bank(g, "gate", s), scalar=1.0, in1=pairs_of(live[g]["u", s][:]),
                op0=ALU.add, op1=ALU.mult,
            )
            live[g]["w", s] = w

        def Z_(g, s):
            nc.vector.scalar_tensor_tensor(
                out=result_block(g, s), in0=live[g]["w", s][:], scalar=0.5, in1=hx_block(g, s), op0=ALU.mult, op1=ALU.add
            )

        warm(3)
        turn("ff2", None, 0); turn("ff2", None, 1)
        warm(2)
        regroup("ff2", None, 0, on_scalar); regroup("ff2", None, 1, on_vector)
        turn("ff1", 0, 0); turn("ff1", 0, 1)
        regroup("ff1", 0, 0, on_scalar); regroup("ff1", 0, 1, on_vector)
        quantise("ff2", None)
        quantise("ff1", 0)
        warm(2)
        turn("in", None, 0); turn("in", None, 1)
        regroup("in", None, 0, on_scalar)
        regroup("in", None, 1, on_vector)
        turn("x", 0, 0); turn("x", 0, 1)
        spread_biases()
        multiply("f", 0)
        regroup("x", 0, 0, on_scalar)
        regroup("x", 0, 1, on_vector)
        quantise("in", None)
        finish_biases()
        quantise("x", 0)
        halve_gate_bias()
        activate("f", 0)
        turn("r", None, 0); turn("r", None, 1)
        multiply("i", 0)
        turn("hx", 0, 0); turn("hx", 0, 1)
        regroup("r", None, 0, on_vector); regroup("r", None, 1, on_vector)
        activate("i", 0, (0, 1, 2))
        regroup("hx", 0, 0, on_scalar)
        activate("i", 0, (3,))
        interleave(0)
        regroup("hx", 0, 1, on_vector)
        quantise("r", None)
        quantise("hx", 0)
        turn("ta", None, 0); turn("ta", None, 1); turn("tb", None, 0); turn("tb", None, 1)
        regroup("ta", None, 0, on_scalar); regroup("ta", None, 1, on_scalar)
        quantise("h", 0)
        regroup("tb", None, 0, on_scalar); regroup("tb", None, 1, on_vector)
        quantise("ta", None); quantise("tb", None)
        for g in range(N_GROUPS):
            n = g + 1
            last = n == N_GROUPS
            if g > 0:
                multiply("f", g)
                activate("f", g)
                turn("hx", g, 0); turn("hx", g, 1)
                regroup("hx", g, 0, on_scalar); regroup("hx", g, 1, on_scalar if last else on_vector)
                interleave(g)
                quantise("hx", g)
                quantise("h", g)
                multiply("i", g)
                activate("i", g)
            if g + 2 < N_GROUPS:
                load_group(g + 2)
            if last:
                B_(g - 1, 0); B_(g - 1, 1)
                E_(g - 1, 0)
            subtract(g, slice(1, 4) if 0 < g < N_GROUPS - 1 else ALL)
            if not last:
                turn("ff1", n, 0); turn("ff1", n, 1); turn("x", n, 0); turn("x", n, 1)
                regroup("ff1", n, 0, on_scalar); regroup("ff1", n, 1, on_scalar)
                quantise("ff1", n)
                regroup("x", n, 0, on_scalar); regroup("x", n, 1, on_scalar)
                if g == 0:
                    quantise("x", n)
            multiply("r", g)
            activate("r", g)
            if g > 0:
                if not last:
                    subtract(g, slice(0, 1))
                    add(g, slice(0, 1), nc.gpsimd)
                    B_(g - 1, 0); E_(g - 1, 0); B_(g - 1, 1); E_(g - 1, 1)
                    B_(g - 1, 3); E_(g - 1, 3)
                    BX_(g - 1, 2); EA_(g - 1, 2)
                    store_blocks(g - 1, 0, BLOCKS)
                    add(g, slice(1, 4), nc.vector)
                    quantise("x", n)
            else:
                add(g, ALL, nc.vector)
            if last:
                E_(g - 1, 1)
                store_blocks(g - 1, 0, 2)
                add(g, ALL, nc.vector)
            multiply("t", g)
            if last:
                BX_(g - 1, 2); BX_(g - 1, 3)
            activate("t", g)
            if not last:
                gate(g, ALL)
        g = N_GROUPS - 1
        EA_(g - 1, 2)
        EA_(g - 1, 3)
        store_blocks(g - 1, 2, BLOCKS)
        for s in range(BLOCKS - 1):
            gate_block(g, s)
            BX_(g, s, 4 if s == 0 else 0)
        gate_block(g, 3)
        B_(g, 3)
        for s in range(BLOCKS - 1):
            EA_(g, s)
            store_blocks(g, s, s + 1)
        E_(g, 3)
        store_blocks(g, 3, 4)
